import numpy as np
import ml_dtypes


def mxq(x, axis, fmt="e4m3"):
    dtype, down = {"e4m3": (ml_dtypes.float8_e4m3fn, 7), "e5m2": (ml_dtypes.float8_e5m2, 14)}[fmt]
    v = np.moveaxis(np.asarray(x, np.float32).astype(ml_dtypes.bfloat16).astype(np.float64), axis, -1)
    blocks = v.reshape(v.shape[:-1] + (-1, 32))
    amax = np.abs(blocks).max(-1, keepdims=True)
    byte = np.maximum(np.where(amax > 0, np.frexp(amax)[1] - 1 + 127, 0) - down, 1)
    scale = np.exp2(byte - 127.0)
    codes = (blocks / scale).astype(np.float32).astype(dtype).astype(np.float64)
    return np.moveaxis((codes * scale).reshape(v.shape), -1, axis)


WIDE = False


def mx_kscale(k):
    if not WIDE:
        return np.ones(k)
    levels = np.array([10, -10, 5, -5, 0])
    a = np.random.permutation(np.resize(levels, k // 512 * 4)).reshape(k // 512, 4)
    idx = np.arange(k)
    return np.exp2(a[idx // 512, idx % 128 // 32])


BF16 = ml_dtypes.bfloat16


def bf(x):
    return np.asarray(x, np.float32).astype(BF16)


def f64(x):
    return np.asarray(x).astype(np.float64)


B, H, N, D, W = 1, 8, 2048, 128, 512
NB = N // W
SCALE = 0.125
MXB = 32


def pad(x, fill):
    return np.concatenate([np.full_like(x[:, :, :1], fill), x], axis=2)


def setup_inputs():
    a = np.sqrt(2.0 / (SCALE * np.sqrt(D)))
    p = np.array(mx_kscale(W), dtype=np.float64)
    p[:MXB] = p.max()
    t = np.tile(p, NB)
    q = np.random.standard_normal((B, H, N, D)) * a
    k = np.random.standard_normal((B, H, N, D)) * a
    v = np.random.standard_normal((B, H, N, D)) * 1.5
    q[..., 0] = 1.0 / SCALE
    k[..., 0] = np.random.standard_normal((B, H, N)) * 0.5 + np.log(t)
    v = v * (t.mean() / t)[:, None]
    return {"q": bf(q), "k": bf(k), "v": bf(v)}


def reference(q, k, v):
    qb = f64(q).reshape(B, H, NB, W, D)
    kt = f64(k).reshape(B, H, NB, W, D).transpose(0, 1, 2, 4, 3)
    i = np.arange(W)
    low = i[None, :] <= i[:, None]
    s1 = np.where(low, (qb @ kt) * SCALE, -np.inf)
    s0 = np.where(low, -np.inf, (qb[:, :, 1:] @ kt[:, :, :-1]) * SCALE)
    m = np.maximum(s1.max(-1, keepdims=True), pad(s0.max(-1, keepdims=True), -np.inf))
    e1 = np.exp(s1 - m)
    e0 = np.exp(s0 - m[:, :, 1:])
    den = e1.sum(-1, keepdims=True) + pad(e0.sum(-1, keepdims=True), 0.0)
    vq = mxq(f64(v), 2, "e4m3").reshape(B, H, NB, W, D)
    num = (mxq(e1, 4, "e4m3") @ vq) + pad(mxq(e0, 4, "e4m3") @ vq[:, :, :-1], 0.0)
    return (num / den).reshape(B, H, N, D)

@@ -1,0 +1,302 @@
+from contextlib import ExitStack
+
+import concourse.mybir as mybir
+from concourse.masks import make_identity
+
+FP8X4 = mybir.dt.float8_e4m3fn_x4
+BF16 = mybir.dt.bfloat16
+F32 = mybir.dt.float32
+I32 = mybir.dt.int32
+U32 = mybir.dt.uint32
+U8 = mybir.dt.uint8
+ALU = mybir.AluOpType
+ACTF = mybir.ActivationFunctionType
+AX = mybir.AxisListType
+
+H = 8
+N = 2048
+D = 128
+W = 512
+P = 128
+NB = N // W
+TPB = W // P
+Q = P // TPB
+SCALE = 0.125
+NEG = -(2.0 ** 100)
+FLOPS = 2 * 2 * H * (2 * NB - 1) * W * W * D
+MANUAL = False
+N_EW = 4
+
+
+def tile_slidingwindowattention_kernel(tc, q, k, v, out):
+    nc = tc.nc
+    with ExitStack() as ctx:
+        const = ctx.enter_context(tc.tile_pool(name="const", bufs=1))
+        raw = ctx.enter_context(tc.tile_pool(name="raw", bufs=3))
+        tpose = ctx.enter_context(tc.tile_pool(name="tpose", bufs=2))
+        vpool = ctx.enter_context(tc.tile_pool(name="vpool", bufs=2))
+        elpool = ctx.enter_context(tc.tile_pool(name="elpool", bufs=2))
+        gpool = ctx.enter_context(tc.tile_pool(name="gpool", bufs=4))
+        cpool = ctx.enter_context(tc.tile_pool(name="cpool", bufs=12))
+        small = ctx.enter_context(tc.tile_pool(name="small", bufs=6))
+        opool = ctx.enter_context(tc.tile_pool(name="opool", bufs=3))
+        ps_w = ctx.enter_context(tc.psum_pool(name="ps_w", bufs=3))
+        ps_l = ctx.enter_context(tc.psum_pool(name="ps_l", bufs=2))
+        ps_m = ctx.enter_context(tc.psum_pool(name="ps_m", bufs=3))
+
+        def zero(t, pattern):
+            nc.vector.memset(t[:].rearrange(pattern).bitcast(I32), 0)
+
+        ident = const.tile([P, P], BF16)
+        make_identity(nc, ident[:])
+        mask_f = const.tile([P, 2, P], F32)
+        nc.gpsimd.memset(mask_f[:], 0.0)
+        nc.gpsimd.affine_select(
+            out=mask_f[:, 0, :], in_=mask_f[:, 0, :], compare_op=ALU.is_ge, fill=NEG,
+            base=0, pattern=[[-1, 4], [-4, Q]], channel_multiplier=1,
+        )
+        nc.gpsimd.affine_select(
+            out=mask_f[:, 1, :], in_=mask_f[:, 1, :], compare_op=ALU.is_ge, fill=NEG,
+            base=-1, pattern=[[1, 4], [4, Q]], channel_multiplier=-1,
+        )
+        mask = const.tile([P, 2, 4, Q], BF16)
+        nc.vector.tensor_copy(out=mask[:].rearrange("p m t c -> p m (t c)"), in_=mask_f[:])
+
+        ew_tiles = []
+        for i in range(N_EW):
+            ew0 = const.tile([P, 4, P], BF16, name="ew%d" % i)
+            zero(ew0, "p t c -> p (t c)")
+            ew_tiles.append(ew0)
+        vsets = []
+        for i in range(2):
+            vset = {
+                "vq": const.tile([P, NB, D], U32, name="vq%d" % i, align_bytes=64),
+                "vs": const.tile([P, NB, D], U8, name="vs%d" % i, align_bytes=64),
+                "vwc": const.tile([P, TPB - 1, NB, D], U32, name="vwc%d" % i, align_bytes=64),
+                "vws": const.tile([P, TPB - 1, NB, D], U8, name="vws%d" % i, align_bytes=64),
+                "vbc": const.tile([P, NB - 1, TPB, D], U32, name="vbc%d" % i, align_bytes=64),
+                "vbs": const.tile([P, NB - 1, TPB, D], U8, name="vbs%d" % i, align_bytes=64),
+            }
+            zero(vset["vs"], "p b d -> p (b d)")
+            for nm in ("vwc", "vws", "vbc", "vbs"):
+                zero(vset[nm], "p a b d -> p (a b d)")
+            vsets.append(vset)
+
+        heads = {}
+
+        def load(h):
+            qr = raw.tile([P, N // P, D], BF16, tag="qr")
+            kr = raw.tile([P, N // P, D], BF16, tag="kr")
+            vr = raw.tile([P, N // P, D], BF16, tag="vr")
+            nc.sync.dma_start(out=qr[:], in_=q[0, h].rearrange("(g p) d -> p g d", p=P))
+            nc.sync.dma_start(out=kr[:].rearrange("p (b t) d -> p b (t d)", t=4), in_=k[0, h].rearrange("(b p t) d -> p b (t d)", p=P, t=4))
+            nc.sync.dma_start(out=vr[:].rearrange("p (b t) d -> p b (t d)", t=4), in_=v[0, h].rearrange("(b p t) d -> p b (t d)", p=P, t=4))
+            qT = tpose.tile([P, N], BF16, tag="qT")
+            kT = tpose.tile([P, N], BF16, tag="kT")
+            heads[h] = {"qr": qr, "kr": kr, "vr": vr, "qT": qT, "kT": kT}
+
+        def prep_qk(h, which, half):
+            src = heads[h]["qr" if which == 0 else "kr"]
+            dst = heads[h]["qT" if which == 0 else "kT"]
+            pt = ps_m.tile([P, 8 * P], BF16, tag="misc")
+            for i in range(8):
+                nc.tensor.transpose(pt[:, i * P:(i + 1) * P], src[:, 8 * half + i, :], ident[:])
+            if which == 0:
+                nc.vector.tensor_copy(out=dst[:, 1024 * half:1024 * (half + 1)], in_=pt[:])
+            else:
+                nc.scalar.copy(out=dst[:, 1024 * half:1024 * (half + 1)], in_=pt[:])
+
+        def prep_v(h):
+            vr = heads[h]["vr"]
+            vset = vsets[h % 2]
+            vg = vpool.tile([P, NB, D, 4], BF16, tag="vg", align_bytes=64)
+            nc.vector.tensor_copy(out=vg[:], in_=vr[:].rearrange("p (b t) d -> p b d t", t=4))
+            nc.vector.quantize_mx(
+                out=vset["vq"][:].rearrange("p b d -> p (b d)").bitcast(FP8X4),
+                scales=vset["vs"][:].rearrange("p b d -> p (b d)"),
+                in_=vg[:].rearrange("p b d t -> p (b d t)"),
+            )
+            for src_n, win_n, bd_n in (("vq", "vwc", "vbc"), ("vs", "vws", "vbs")):
+                src = vset[src_n][:].bitcast(I32)
+                win = vset[win_n][:].bitcast(I32)
+                bd = vset[bd_n][:].bitcast(I32)
+                for r in range(TPB - 1):
+                    cut = Q * (r + 1)
+                    nc.sync.dma_start(out=win[0:cut, r, :, :], in_=src[0:cut, :, :])
+                    nc.sync.dma_start(out=win[cut:P, r, 1:NB, :], in_=src[cut:P, 0:NB - 1, :])
+                for s in range(TPB):
+                    nc.sync.dma_start(out=bd[Q * s:Q * (s + 1), :, s, :], in_=src[Q * s:Q * (s + 1), 0:NB - 1, :])
+
+        tiles = [(h, j, r) for h in range(H) for j in range(NB) for r in range(TPB)]
+        st = {}
+
+        def s_lead(h, j):
+            hd = heads[h]
+            kTv = hd["kT"][:].rearrange("d (b t c) -> d b t c", t=4, c=P)
+            sl = ps_l.tile([P, TPB, 4, Q], F32, tag="sl")
+            for r in range(TPB):
+                i = TPB * j + r
+                nc.tensor.matmul(sl[:, r, :, :], lhsT=hd["qT"][:, i * P:(i + 1) * P], rhs=kTv[:, j - 1, :, Q * r:Q * (r + 1)], start=True, stop=False)
+                nc.tensor.matmul(sl[:, r, :, :], lhsT=ident[:], rhs=mask[:, 1, :, :], start=False, stop=True)
+            st[("sl", h, j)] = sl
+            st[("el", h, j)] = elpool.tile([P, 4, P], BF16, tag="el", name="el")
+
+        def s_win(x):
+            h, j, r = tiles[x]
+            hd = heads[h]
+            if r == 0:
+                st[("den", h, j)] = small.tile([P, TPB, 2], F32, tag="den", name="den")
+                if j > 0:
+                    s_lead(h, j)
+            kTv = hd["kT"][:].rearrange("d (b t c) -> d b t c", t=4, c=P)
+            i = TPB * j + r
+            qcols = hd["qT"][:, i * P:(i + 1) * P]
+            cut = Q * (r + 1)
+            sw = ps_w.tile([P, 4, P], F32, tag="sw")
+            nc.tensor.matmul(sw[:, :, 0:cut], lhsT=qcols, rhs=kTv[:, j, :, 0:cut], start=True, stop=False)
+            if j > 0 and cut < P:
+                nc.tensor.matmul(sw[:, :, cut:P], lhsT=qcols, rhs=kTv[:, j - 1, :, cut:P], start=False, stop=False)
+            nc.tensor.matmul(sw[:, :, cut - Q:cut], lhsT=ident[:], rhs=mask[:, 0, :, :], start=False, stop=True)
+            st[("sw", x)] = sw
+
+        def seen(x):
+            h, j, r = tiles[x]
+            return P if j > 0 else Q * (r + 1)
+
+        def row_max(x):
+            h, j, r = tiles[x]
+            sw = st[("sw", x)]
+            m2 = small.tile([P, 2], F32, tag="m2")
+            nb = small.tile([P, 1], F32, tag="nb")
+            nc.vector.tensor_reduce(out=m2[:, 0:1], in_=sw[:, :, 0:seen(x)], axis=AX.XY, op=ALU.max)
+            if j > 0:
+                nc.vector.tensor_reduce(out=m2[:, 1:2], in_=st[("sl", h, j)][:, r, :, :], axis=AX.XY, op=ALU.max)
+                nc.vector.tensor_scalar(out=nb[:], in0=m2[:, 0:1], scalar1=m2[:, 1:2], scalar2=-SCALE, op0=ALU.max, op1=ALU.mult)
+            else:
+                nc.vector.tensor_scalar(out=nb[:], in0=m2[:, 0:1], scalar1=-SCALE, scalar2=None, op0=ALU.mult)
+            st[("nb", x)] = nb
+
+        def expo(x):
+            h, j, r = tiles[x]
+            sw = st[("sw", x)]
+            nb = st[("nb", x)]
+            den = st[("den", h, j)]
+            ew = ew_tiles[x % N_EW]
+            nc.scalar.activation(out=ew[:, :, 0:seen(x)], in_=sw[:, :, 0:seen(x)], func=ACTF.Exp, bias=nb[:], scale=SCALE, accum_out=den[:, r, 0:1])
+            if j > 0:
+                nc.scalar.activation(
+                    out=st[("el", h, j)][:, :, Q * r:Q * (r + 1)], in_=st[("sl", h, j)][:, r, :, :],
+                    func=ACTF.Exp, bias=nb[:], scale=SCALE, accum_out=den[:, r, 1:2])
+
+        def flip(key, src):
+            et = ps_m.tile([P, 4, P], BF16, tag="misc", name="et")
+            for t in range(4):
+                nc.tensor.transpose(et[:, t, :], src[:, t, :], ident[:])
+            st[("et",) + key] = et
+
+        def evict(key, on_scalar):
+            et = st[("et",) + key]
+            g = gpool.tile([P, P, 4], BF16, tag="g", align_bytes=64)
+            if on_scalar:
+                nc.scalar.copy(out=g[:], in_=et[:].rearrange("p t n -> p n t"))
+            else:
+                nc.vector.tensor_copy(out=g[:], in_=et[:].rearrange("p t n -> p n t"))
+            st[("g",) + key] = g
+
+        def quant(key):
+            g = st[("g",) + key]
+            codes = cpool.tile([P, P], U32, tag="codes", align_bytes=64)
+            scl = cpool.tile([P, P], U8, tag="scl", align_bytes=64)
+            nc.vector.quantize_mx(out=codes[:].bitcast(FP8X4), scales=scl[:], in_=g[:].rearrange("p n t -> p (n t)"))
+            st[("c",) + key] = (codes, scl)
+
+        def mx(h, j):
+            vset = vsets[h % 2]
+            acc = ps_m.tile([P, TPB, D], F32, tag="misc", name="acc")
+            for r in range(TPB):
+                codes, scl = st[("c", "w", h, j, r)]
+                if r < TPB - 1:
+                    rhs, rsc = vset["vwc"][:, r, j, :], vset["vws"][:, r, j, :]
+                else:
+                    rhs, rsc = vset["vq"][:, j, :], vset["vs"][:, j, :]
+                nc.tensor.matmul_mx(
+                    out=acc[:, r, :], lhsT=codes[:].bitcast(FP8X4), lhsT_scale=scl[:],
+                    rhs=rhs.bitcast(FP8X4), rhs_scale=rsc,
+                    start=(r == 0), stop=(j == 0 and r == TPB - 1))
+            if j > 0:
+                codes, scl = st[("c", "l", h, j)]
+                nc.tensor.matmul_mx(
+                    out=acc[:].rearrange("p r d -> p (r d)"), lhsT=codes[:].bitcast(FP8X4), lhsT_scale=scl[:],
+                    rhs=vset["vbc"][:, j - 1, :, :].rearrange("p s d -> p (s d)").bitcast(FP8X4),
+                    rhs_scale=vset["vbs"][:, j - 1, :, :].rearrange("p s d -> p (s d)"),
+                    start=False, stop=True)
+            st[("acc", h, j)] = acc
+
+        def fin(h, j):
+            acc = st[("acc", h, j)]
+            den = st[("den", h, j)]
+            rden = small.tile([P, TPB], F32, tag="rden")
+            if j > 0:
+                dsum = small.tile([P, TPB], F32, tag="dsum")
+                nc.vector.tensor_reduce(out=dsum[:], in_=den[:], axis=AX.X, op=ALU.add)
+                nc.vector.reciprocal(out=rden[:], in_=dsum[:])
+            else:
+                nc.vector.reciprocal(out=rden[:], in_=den[:, :, 0])
+            res = opool.tile([P, TPB, D], F32, tag="res")
+            nc.vector.tensor_tensor(out=res[:], in0=acc[:], in1=rden[:].unsqueeze(2).to_broadcast([P, TPB, D]), op=ALU.mult)
+            nc.gpsimd.dma_start(out=out[0, h, j * W:(j + 1) * W, :].rearrange("(r p) d -> p r d", p=P), in_=res[:])
+
+        def ok(x):
+            return 0 <= x < len(tiles)
+
+        def slot(s):
+            x = s - 3
+            if ok(x):
+                h, j, r = tiles[x]
+                evict(("w", h, j, r), r < TPB - 1)
+                if r == TPB - 1 and j > 0:
+                    evict(("l", h, j), j % 2 == 1)
+            x = s - 4
+            if ok(x):
+                h, j, r = tiles[x]
+                quant(("w", h, j, r))
+                if r == TPB - 1 and j > 0:
+                    quant(("l", h, j))
+            if ok(s + 1):
+                s_win(s + 1)
+            if ok(s):
+                row_max(s)
+            if ok(s - 1):
+                expo(s - 1)
+            x = s - 2
+            if ok(x):
+                h, j, r = tiles[x]
+                flip(("w", h, j, r), ew_tiles[x % N_EW])
+                if r == TPB - 1 and j > 0:
+                    flip(("l", h, j), st[("el", h, j)])
+            x = s - 4
+            if ok(x) and tiles[x][2] == TPB - 1:
+                mx(tiles[x][0], tiles[x][1])
+            x = s - 5
+            if ok(x) and tiles[x][2] == TPB - 1:
+                fin(tiles[x][0], tiles[x][1])
+            if ok(s):
+                h, j, r = tiles[s]
+                if (j, r) == (0, 0) and h + 2 < H:
+                    load(h + 2)
+                if h + 1 < H:
+                    if r == 1:
+                        prep_qk(h + 1, j % 2, j // 2)
+                    if (j, r) == (1, 2):
+                        prep_v(h + 1)
+
+        load(0)
+        load(1)
+        for step in range(4):
+            prep_qk(0, step % 2, step // 2)
+        prep_v(0)
+        if MANUAL:
+            ctx.enter_context(tc.manual_schedule())
+        s_win(0)
+        for s in range(len(tiles) + 6):
+            slot(s)

@@ -37,6 +37,7 @@ def tile_slidingwindowattention_kernel(tc, q, k, v, out):
         vpool = ctx.enter_context(tc.tile_pool(name="vpool", bufs=2))
         elpool = ctx.enter_context(tc.tile_pool(name="elpool", bufs=2))
         gpool = ctx.enter_context(tc.tile_pool(name="gpool", bufs=4))
+        ppool = ctx.enter_context(tc.tile_pool(name="ppool", bufs=4))
         cpool = ctx.enter_context(tc.tile_pool(name="cpool", bufs=12))
         small = ctx.enter_context(tc.tile_pool(name="small", bufs=6))
         opool = ctx.enter_context(tc.tile_pool(name="opool", bufs=3))
@@ -91,12 +92,12 @@ def tile_slidingwindowattention_kernel(tc, q, k, v, out):
             nc.sync.dma_start(out=qr[:], in_=q[0, h].rearrange("(g p) d -> p g d", p=P))
             nc.sync.dma_start(out=kr[:].rearrange("p (b t) d -> p b (t d)", t=4), in_=k[0, h].rearrange("(b p t) d -> p b (t d)", p=P, t=4))
             nc.sync.dma_start(out=vr[:].rearrange("p (b t) d -> p b (t d)", t=4), in_=v[0, h].rearrange("(b p t) d -> p b (t d)", p=P, t=4))
-            qT = tpose.tile([P, N], BF16, tag="qT")
-            kT = tpose.tile([P, N], BF16, tag="kT")
-            heads[h] = {"qr": qr, "kr": kr, "vr": vr, "qT": qT, "kT": kT}
+            heads[h] = {"qr": qr, "kr": kr, "vr": vr}
 
         def prep_qk(h, which, half):
             src = heads[h]["qr" if which == 0 else "kr"]
+            if half == 0:
+                heads[h]["qT" if which == 0 else "kT"] = tpose.tile([P, N], BF16, tag="qT" if which == 0 else "kT", name="xT")
             dst = heads[h]["qT" if which == 0 else "kT"]
             pt = ps_m.tile([P, 8 * P], BF16, tag="misc")
             for i in range(8):
@@ -196,11 +197,17 @@ def tile_slidingwindowattention_kernel(tc, q, k, v, out):
 
         def evict(key, on_scalar):
             et = st[("et",) + key]
-            g = gpool.tile([P, P, 4], BF16, tag="g", align_bytes=64)
+            pl = ppool.tile([P, 4, P], BF16, tag="pl")
             if on_scalar:
-                nc.scalar.copy(out=g[:], in_=et[:].rearrange("p t n -> p n t"))
+                nc.scalar.copy(out=pl[:], in_=et[:])
             else:
-                nc.vector.tensor_copy(out=g[:], in_=et[:].rearrange("p t n -> p n t"))
+                nc.vector.tensor_copy(out=pl[:], in_=et[:])
+            st[("pl",) + key] = pl
+
+        def regroup(key):
+            pl = st[("pl",) + key]
+            g = gpool.tile([P, P, 4], BF16, tag="g", align_bytes=64)
+            nc.gpsimd.tensor_scalar(out=g[:], in0=pl[:].rearrange("p t n -> p n t"), scalar1=1.0, scalar2=0.0, op0=ALU.mult, op1=ALU.add)
             st[("g",) + key] = g
 
         def quant(key):
@@ -244,7 +251,7 @@ def tile_slidingwindowattention_kernel(tc, q, k, v, out):
                 nc.vector.reciprocal(out=rden[:], in_=den[:, :, 0])
             res = opool.tile([P, TPB, D], F32, tag="res")
             nc.vector.tensor_tensor(out=res[:], in0=acc[:], in1=rden[:].unsqueeze(2).to_broadcast([P, TPB, D]), op=ALU.mult)
-            nc.gpsimd.dma_start(out=out[0, h, j * W:(j + 1) * W, :].rearrange("(r p) d -> p r d", p=P), in_=res[:])
+            nc.sync.dma_start(out=out[0, h, j * W:(j + 1) * W, :].rearrange("(r p) d -> p r d", p=P), in_=res[:])
 
         def ok(x):
             return 0 <= x < len(tiles)
@@ -253,10 +260,12 @@ def tile_slidingwindowattention_kernel(tc, q, k, v, out):
             x = s - 3
             if ok(x):
                 h, j, r = tiles[x]
-                evict(("w", h, j, r), r < TPB - 1)
+                evict(("w", h, j, r), True)
+                regroup(("w", h, j, r))
                 if r == TPB - 1 and j > 0:
-                    evict(("l", h, j), j % 2 == 1)
-            x = s - 4
+                    evict(("l", h, j), False)
+                    regroup(("l", h, j))
+            x = s - 5
             if ok(x):
                 h, j, r = tiles[x]
                 quant(("w", h, j, r))
@@ -274,10 +283,10 @@ def tile_slidingwindowattention_kernel(tc, q, k, v, out):
                 flip(("w", h, j, r), ew_tiles[x % N_EW])
                 if r == TPB - 1 and j > 0:
                     flip(("l", h, j), st[("el", h, j)])
-            x = s - 4
+            x = s - 5
             if ok(x) and tiles[x][2] == TPB - 1:
                 mx(tiles[x][0], tiles[x][1])
-            x = s - 5
+            x = s - 6
             if ok(x) and tiles[x][2] == TPB - 1:
                 fin(tiles[x][0], tiles[x][1])
             if ok(s):
@@ -298,5 +307,5 @@ def tile_slidingwindowattention_kernel(tc, q, k, v, out):
         if MANUAL:
             ctx.enter_context(tc.manual_schedule())
         s_win(0)
-        for s in range(len(tiles) + 6):
+        for s in range(len(tiles) + 7):
             slot(s)

@@ -24,7 +24,7 @@ Q = P // TPB
 SCALE = 0.125
 NEG = -(2.0 ** 100)
 FLOPS = 2 * 2 * H * (2 * NB - 1) * W * W * D
-MANUAL = False
+MANUAL = True
 N_EW = 4
 
 
@@ -37,7 +37,6 @@ def tile_slidingwindowattention_kernel(tc, q, k, v, out):
         vpool = ctx.enter_context(tc.tile_pool(name="vpool", bufs=2))
         elpool = ctx.enter_context(tc.tile_pool(name="elpool", bufs=2))
         gpool = ctx.enter_context(tc.tile_pool(name="gpool", bufs=4))
-        ppool = ctx.enter_context(tc.tile_pool(name="ppool", bufs=4))
         cpool = ctx.enter_context(tc.tile_pool(name="cpool", bufs=12))
         small = ctx.enter_context(tc.tile_pool(name="small", bufs=6))
         opool = ctx.enter_context(tc.tile_pool(name="opool", bufs=3))
@@ -197,17 +196,11 @@ def tile_slidingwindowattention_kernel(tc, q, k, v, out):
 
         def evict(key, on_scalar):
             et = st[("et",) + key]
-            pl = ppool.tile([P, 4, P], BF16, tag="pl")
-            if on_scalar:
-                nc.scalar.copy(out=pl[:], in_=et[:])
-            else:
-                nc.vector.tensor_copy(out=pl[:], in_=et[:])
-            st[("pl",) + key] = pl
-
-        def regroup(key):
-            pl = st[("pl",) + key]
             g = gpool.tile([P, P, 4], BF16, tag="g", align_bytes=64)
-            nc.gpsimd.tensor_scalar(out=g[:], in0=pl[:].rearrange("p t n -> p n t"), scalar1=1.0, scalar2=0.0, op0=ALU.mult, op1=ALU.add)
+            if on_scalar:
+                nc.scalar.copy(out=g[:], in_=et[:].rearrange("p t n -> p n t"))
+            else:
+                nc.vector.tensor_copy(out=g[:], in_=et[:].rearrange("p t n -> p n t"))
             st[("g",) + key] = g
 
         def quant(key):
@@ -251,7 +244,7 @@ def tile_slidingwindowattention_kernel(tc, q, k, v, out):
                 nc.vector.reciprocal(out=rden[:], in_=den[:, :, 0])
             res = opool.tile([P, TPB, D], F32, tag="res")
             nc.vector.tensor_tensor(out=res[:], in0=acc[:], in1=rden[:].unsqueeze(2).to_broadcast([P, TPB, D]), op=ALU.mult)
-            nc.sync.dma_start(out=out[0, h, j * W:(j + 1) * W, :].rearrange("(r p) d -> p r d", p=P), in_=res[:])
+            nc.gpsimd.dma_start(out=out[0, h, j * W:(j + 1) * W, :].rearrange("(r p) d -> p r d", p=P), in_=res[:])
 
         def ok(x):
             return 0 <= x < len(tiles)
@@ -260,12 +253,10 @@ def tile_slidingwindowattention_kernel(tc, q, k, v, out):
             x = s - 3
             if ok(x):
                 h, j, r = tiles[x]
-                evict(("w", h, j, r), True)
-                regroup(("w", h, j, r))
+                evict(("w", h, j, r), r < TPB - 1)
                 if r == TPB - 1 and j > 0:
-                    evict(("l", h, j), False)
-                    regroup(("l", h, j))
-            x = s - 5
+                    evict(("l", h, j), j % 2 == 1)
+            x = s - 4
             if ok(x):
                 h, j, r = tiles[x]
                 quant(("w", h, j, r))
@@ -283,10 +274,10 @@ def tile_slidingwindowattention_kernel(tc, q, k, v, out):
                 flip(("w", h, j, r), ew_tiles[x % N_EW])
                 if r == TPB - 1 and j > 0:
                     flip(("l", h, j), st[("el", h, j)])
-            x = s - 5
+            x = s - 4
             if ok(x) and tiles[x][2] == TPB - 1:
                 mx(tiles[x][0], tiles[x][1])
-            x = s - 6
+            x = s - 5
             if ok(x) and tiles[x][2] == TPB - 1:
                 fin(tiles[x][0], tiles[x][1])
             if ok(s):
@@ -307,5 +298,5 @@ def tile_slidingwindowattention_kernel(tc, q, k, v, out):
         if MANUAL:
             ctx.enter_context(tc.manual_schedule())
         s_win(0)
-        for s in range(len(tiles) + 7):
+        for s in range(len(tiles) + 6):
             slot(s)

@@ -24,7 +24,7 @@ Q = P // TPB
 SCALE = 0.125
 NEG = -(2.0 ** 100)
 FLOPS = 2 * 2 * H * (2 * NB - 1) * W * W * D
-MANUAL = True
+MANUAL = False
 N_EW = 4
 
 
@@ -88,9 +88,15 @@ def tile_slidingwindowattention_kernel(tc, q, k, v, out):
             qr = raw.tile([P, N // P, D], BF16, tag="qr")
             kr = raw.tile([P, N // P, D], BF16, tag="kr")
             vr = raw.tile([P, N // P, D], BF16, tag="vr")
-            nc.sync.dma_start(out=qr[:], in_=q[0, h].rearrange("(g p) d -> p g d", p=P))
-            nc.sync.dma_start(out=kr[:].rearrange("p (b t) d -> p b (t d)", t=4), in_=k[0, h].rearrange("(b p t) d -> p b (t d)", p=P, t=4))
-            nc.sync.dma_start(out=vr[:].rearrange("p (b t) d -> p b (t d)", t=4), in_=v[0, h].rearrange("(b p t) d -> p b (t d)", p=P, t=4))
+            q_rows = q[0, h].rearrange("(g p) d -> p g d", p=P)
+            k_rows = k[0, h].rearrange("(b p t) d -> p b (t d)", p=P, t=4)
+            v_rows = v[0, h].rearrange("(b p t) d -> p b (t d)", p=P, t=4)
+            kr4 = kr[:].rearrange("p (b t) d -> p b (t d)", t=4)
+            nc.sync.dma_start(out=qr[:, 0:8, :], in_=q_rows[:, 0:8, :])
+            nc.sync.dma_start(out=kr4[:, 0:2, :], in_=k_rows[:, 0:2, :])
+            nc.sync.dma_start(out=vr[:].rearrange("p (b t) d -> p b (t d)", t=4), in_=v_rows)
+            nc.sync.dma_start(out=qr[:, 8:16, :], in_=q_rows[:, 8:16, :])
+            nc.sync.dma_start(out=kr4[:, 2:4, :], in_=k_rows[:, 2:4, :])
             heads[h] = {"qr": qr, "kr": kr, "vr": vr}
 
         def prep_qk(h, which, half):
@@ -171,9 +177,9 @@ def tile_slidingwindowattention_kernel(tc, q, k, v, out):
             nc.vector.tensor_reduce(out=m2[:, 0:1], in_=sw[:, :, 0:seen(x)], axis=AX.XY, op=ALU.max)
             if j > 0:
                 nc.vector.tensor_reduce(out=m2[:, 1:2], in_=st[("sl", h, j)][:, r, :, :], axis=AX.XY, op=ALU.max)
-                nc.vector.tensor_scalar(out=nb[:], in0=m2[:, 0:1], scalar1=m2[:, 1:2], scalar2=-SCALE, op0=ALU.max, op1=ALU.mult)
+                nc.gpsimd.tensor_scalar(out=nb[:], in0=m2[:, 0:1], scalar1=m2[:, 1:2], scalar2=-SCALE, op0=ALU.max, op1=ALU.mult)
             else:
-                nc.vector.tensor_scalar(out=nb[:], in0=m2[:, 0:1], scalar1=-SCALE, scalar2=None, op0=ALU.mult)
+                nc.gpsimd.tensor_scalar(out=nb[:], in0=m2[:, 0:1], scalar1=-SCALE, scalar2=0.0, op0=ALU.mult, op1=ALU.add)
             st[("nb", x)] = nb
 
         def expo(x):
@@ -238,13 +244,13 @@ def tile_slidingwindowattention_kernel(tc, q, k, v, out):
             rden = small.tile([P, TPB], F32, tag="rden")
             if j > 0:
                 dsum = small.tile([P, TPB], F32, tag="dsum")
-                nc.vector.tensor_reduce(out=dsum[:], in_=den[:], axis=AX.X, op=ALU.add)
+                nc.gpsimd.tensor_tensor(out=dsum[:], in0=den[:, :, 0], in1=den[:, :, 1], op=ALU.add)
                 nc.vector.reciprocal(out=rden[:], in_=dsum[:])
             else:
                 nc.vector.reciprocal(out=rden[:], in_=den[:, :, 0])
             res = opool.tile([P, TPB, D], F32, tag="res")
             nc.vector.tensor_tensor(out=res[:], in0=acc[:], in1=rden[:].unsqueeze(2).to_broadcast([P, TPB, D]), op=ALU.mult)
-            nc.gpsimd.dma_start(out=out[0, h, j * W:(j + 1) * W, :].rearrange("(r p) d -> p r d", p=P), in_=res[:])
+            nc.sync.dma_start(out=out[0, h, j * W:(j + 1) * W, :].rearrange("(r p) d -> p r d", p=P), in_=res[:])
 
         def ok(x):
             return 0 <= x < len(tiles)
@@ -292,9 +298,11 @@ def tile_slidingwindowattention_kernel(tc, q, k, v, out):
 
         load(0)
         load(1)
-        for step in range(4):
+        for step in range(2):
             prep_qk(0, step % 2, step // 2)
         prep_v(0)
+        for step in range(2, 4):
+            prep_qk(0, step % 2, step // 2)
         if MANUAL:
             ctx.enter_context(tc.manual_schedule())
         s_win(0)

@@ -116,7 +116,9 @@ def tile_slidingwindowattention_kernel(tc, q, k, v, out):
             vr = heads[h]["vr"]
             vset = vsets[h % 2]
             vg = vpool.tile([P, NB, D, 4], BF16, tag="vg", align_bytes=64)
-            nc.vector.tensor_copy(out=vg[:], in_=vr[:].rearrange("p (b t) d -> p b d t", t=4))
+            nc.vector.tensor_copy(
+                out=vg[:].rearrange("p b (c i) t -> p b c t i", i=4),
+                in_=vr[:].rearrange("p (b t) (c i) -> p b c t i", t=4, i=4))
             nc.vector.quantize_mx(
                 out=vset["vq"][:].rearrange("p b d -> p (b d)").bitcast(FP8X4),
                 scales=vset["vs"][:].rearrange("p b d -> p (b d)"),
@@ -203,10 +205,12 @@ def tile_slidingwindowattention_kernel(tc, q, k, v, out):
         def evict(key, on_scalar):
             et = st[("et",) + key]
             g = gpool.tile([P, P, 4], BF16, tag="g", align_bytes=64)
+            dst = g[:].rearrange("p (c i) t -> p c t i", i=4)
+            src = et[:].rearrange("p t (c i) -> p c t i", i=4)
             if on_scalar:
-                nc.scalar.copy(out=g[:], in_=et[:].rearrange("p t n -> p n t"))
+                nc.scalar.copy(out=dst, in_=src)
             else:
-                nc.vector.tensor_copy(out=g[:], in_=et[:].rearrange("p t n -> p n t"))
+                nc.vector.tensor_copy(out=dst, in_=src)
             st[("g",) + key] = g
 
         def quant(key):

@@ -40,9 +40,11 @@ def tile_slidingwindowattention_kernel(tc, q, k, v, out):
         cpool = ctx.enter_context(tc.tile_pool(name="cpool", bufs=12))
         small = ctx.enter_context(tc.tile_pool(name="small", bufs=6))
         opool = ctx.enter_context(tc.tile_pool(name="opool", bufs=3))
+        zpool = ctx.enter_context(tc.tile_pool(name="zpool", bufs=6))
+        zlpool = ctx.enter_context(tc.tile_pool(name="zlpool", bufs=3))
         ps_w = ctx.enter_context(tc.psum_pool(name="ps_w", bufs=3))
-        ps_l = ctx.enter_context(tc.psum_pool(name="ps_l", bufs=2))
-        ps_m = ctx.enter_context(tc.psum_pool(name="ps_m", bufs=3))
+        ps_l = ctx.enter_context(tc.psum_pool(name="ps_l", bufs=1))
+        ps_m = ctx.enter_context(tc.psum_pool(name="ps_m", bufs=4))
 
         def zero(t, pattern):
             nc.vector.memset(t[:].rearrange(pattern).bitcast(I32), 0)
@@ -146,7 +148,14 @@ def tile_slidingwindowattention_kernel(tc, q, k, v, out):
                 i = TPB * j + r
                 nc.tensor.matmul(sl[:, r, :, :], lhsT=hd["qT"][:, i * P:(i + 1) * P], rhs=kTv[:, j - 1, :, Q * r:Q * (r + 1)], start=True, stop=False)
                 nc.tensor.matmul(sl[:, r, :, :], lhsT=ident[:], rhs=mask[:, 1, :, :], start=False, stop=True)
-            st[("sl", h, j)] = sl
+            zl = zlpool.tile([P, TPB, 4, Q], F32, tag="zl")
+            nbl = small.tile([P, TPB], F32, tag="nbl")
+            for r in range(TPB):
+                nc.vector.tensor_scalar(
+                    out=zl[:, r, :, :], in0=sl[:, r, :, :], scalar1=-SCALE, scalar2=None,
+                    op0=ALU.mult, op1=ALU.min, accum_out=nbl[:, r:r + 1])
+            st[("zl", h, j)] = zl
+            st[("nbl", h, j)] = nbl
             st[("el", h, j)] = elpool.tile([P, 4, P], BF16, tag="el", name="el")
 
         def s_win(x):
@@ -174,27 +183,26 @@ def tile_slidingwindowattention_kernel(tc, q, k, v, out):
         def row_max(x):
             h, j, r = tiles[x]
             sw = st[("sw", x)]
-            m2 = small.tile([P, 2], F32, tag="m2")
+            zw = zpool.tile([P, 4, P], F32, tag="zw")
             nb = small.tile([P, 1], F32, tag="nb")
-            nc.vector.tensor_reduce(out=m2[:, 0:1], in_=sw[:, :, 0:seen(x)], axis=AX.XY, op=ALU.max)
-            if j > 0:
-                nc.vector.tensor_reduce(out=m2[:, 1:2], in_=st[("sl", h, j)][:, r, :, :], axis=AX.XY, op=ALU.max)
-                nc.gpsimd.tensor_scalar(out=nb[:], in0=m2[:, 0:1], scalar1=m2[:, 1:2], scalar2=-SCALE, op0=ALU.max, op1=ALU.mult)
-            else:
-                nc.gpsimd.tensor_scalar(out=nb[:], in0=m2[:, 0:1], scalar1=-SCALE, scalar2=0.0, op0=ALU.mult, op1=ALU.add)
+            nc.vector.tensor_scalar(
+                out=zw[:, :, 0:seen(x)], in0=sw[:, :, 0:seen(x)], scalar1=-SCALE,
+                scalar2=st[("nbl", h, j)][:, r:r + 1] if j > 0 else None,
+                op0=ALU.mult, op1=ALU.min, accum_out=nb[:])
+            st[("zw", x)] = zw
             st[("nb", x)] = nb
 
         def expo(x):
             h, j, r = tiles[x]
-            sw = st[("sw", x)]
+            zw = st[("zw", x)]
             nb = st[("nb", x)]
             den = st[("den", h, j)]
             ew = ew_tiles[x % N_EW]
-            nc.scalar.activation(out=ew[:, :, 0:seen(x)], in_=sw[:, :, 0:seen(x)], func=ACTF.Exp, bias=nb[:], scale=SCALE, accum_out=den[:, r, 0:1])
+            nc.scalar.activation(out=ew[:, :, 0:seen(x)], in_=zw[:, :, 0:seen(x)], func=ACTF.Exp, bias=nb[:], scale=-1.0, accum_out=den[:, r, 0:1])
             if j > 0:
                 nc.scalar.activation(
-                    out=st[("el", h, j)][:, :, Q * r:Q * (r + 1)], in_=st[("sl", h, j)][:, r, :, :],
-                    func=ACTF.Exp, bias=nb[:], scale=SCALE, accum_out=den[:, r, 1:2])
+                    out=st[("el", h, j)][:, :, Q * r:Q * (r + 1)], in_=st[("zl", h, j)][:, r, :, :],
+                    func=ACTF.Exp, bias=nb[:], scale=-1.0, accum_out=den[:, r, 1:2])
 
         def flip(key, src):
             et = ps_m.tile([P, 4, P], BF16, tag="misc", name="et")

@@ -271,7 +271,7 @@ def tile_slidingwindowattention_kernel(tc, q, k, v, out):
             x = s - 3
             if ok(x):
                 h, j, r = tiles[x]
-                evict(("w", h, j, r), r < TPB - 1)
+                evict(("w", h, j, r), r < TPB - 2)
                 if r == TPB - 1 and j > 0:
                     evict(("l", h, j), j % 2 == 1)
             x = s - 4

@@ -271,7 +271,7 @@ def tile_slidingwindowattention_kernel(tc, q, k, v, out):
             x = s - 3
             if ok(x):
                 h, j, r = tiles[x]
-                evict(("w", h, j, r), r < TPB - 2)
+                evict(("w", h, j, r), r < TPB - 1 or j % 2 == 0)
                 if r == TPB - 1 and j > 0:
                     evict(("l", h, j), j % 2 == 1)
             x = s - 4

@@ -51,23 +51,25 @@ def tile_slidingwindowattention_kernel(tc, q, k, v, out):
 
         ident = const.tile([P, P], BF16)
         make_identity(nc, ident[:])
+        ident_f = const.tile([P, P], F32)
+        make_identity(nc, ident_f[:])
         mask_f = const.tile([P, 2, P], F32)
         nc.gpsimd.memset(mask_f[:], 0.0)
         nc.gpsimd.affine_select(
             out=mask_f[:, 0, :], in_=mask_f[:, 0, :], compare_op=ALU.is_ge, fill=NEG,
-            base=0, pattern=[[-1, 4], [-4, Q]], channel_multiplier=1,
+            base=0, pattern=[[-1, 2], [-4, Q], [-2, 2]], channel_multiplier=1,
         )
         nc.gpsimd.affine_select(
             out=mask_f[:, 1, :], in_=mask_f[:, 1, :], compare_op=ALU.is_ge, fill=NEG,
-            base=-1, pattern=[[1, 4], [4, Q]], channel_multiplier=-1,
+            base=-1, pattern=[[1, 2], [4, Q], [2, 2]], channel_multiplier=-1,
         )
-        mask = const.tile([P, 2, 4, Q], BF16)
-        nc.vector.tensor_copy(out=mask[:].rearrange("p m t c -> p m (t c)"), in_=mask_f[:])
+        mask = const.tile([P, 2, 2, 2 * Q], BF16)
+        nc.vector.tensor_copy(out=mask[:].rearrange("p m u x -> p m (u x)"), in_=mask_f[:])
 
         ew_tiles = []
         for i in range(N_EW):
-            ew0 = const.tile([P, 4, P], BF16, name="ew%d" % i)
-            zero(ew0, "p t c -> p (t c)")
+            ew0 = const.tile([P, 2, 2 * P], BF16, name="ew%d" % i)
+            zero(ew0, "p u x -> p (u x)")
             ew_tiles.append(ew0)
         vsets = []
         for i in range(2):
@@ -91,14 +93,14 @@ def tile_slidingwindowattention_kernel(tc, q, k, v, out):
             kr = raw.tile([P, N // P, D], BF16, tag="kr")
             vr = raw.tile([P, N // P, D], BF16, tag="vr")
             q_rows = q[0, h].rearrange("(g p) d -> p g d", p=P)
-            k_rows = k[0, h].rearrange("(b p t) d -> p b (t d)", p=P, t=4)
+            k_rows = k[0, h].rearrange("(g p s) d -> p g (s d)", p=P, s=2)
             v_rows = v[0, h].rearrange("(b p t) d -> p b (t d)", p=P, t=4)
-            kr4 = kr[:].rearrange("p (b t) d -> p b (t d)", t=4)
+            kr2 = kr[:].rearrange("p (g s) d -> p g (s d)", s=2)
             nc.sync.dma_start(out=qr[:, 0:8, :], in_=q_rows[:, 0:8, :])
-            nc.sync.dma_start(out=kr4[:, 0:2, :], in_=k_rows[:, 0:2, :])
+            nc.sync.dma_start(out=kr2[:, 0:4, :], in_=k_rows[:, 0:4, :])
             nc.sync.dma_start(out=vr[:].rearrange("p (b t) d -> p b (t d)", t=4), in_=v_rows)
             nc.sync.dma_start(out=qr[:, 8:16, :], in_=q_rows[:, 8:16, :])
-            nc.sync.dma_start(out=kr4[:, 2:4, :], in_=k_rows[:, 2:4, :])
+            nc.sync.dma_start(out=kr2[:, 4:8, :], in_=k_rows[:, 4:8, :])
             heads[h] = {"qr": qr, "kr": kr, "vr": vr}
 
         def prep_qk(h, which, half):
@@ -108,7 +110,12 @@ def tile_slidingwindowattention_kernel(tc, q, k, v, out):
             dst = heads[h]["qT" if which == 0 else "kT"]
             pt = ps_m.tile([P, 8 * P], BF16, tag="misc")
             for i in range(8):
-                nc.tensor.transpose(pt[:, i * P:(i + 1) * P], src[:, 8 * half + i, :], ident[:])
+                if which == 0:
+                    slot_i = 8 * half + i
+                else:
+                    b_loc, u, hh = i // 4, (i // 2) % 2, i % 2
+                    slot_i = 8 * half + 2 * (2 * b_loc + hh) + u
+                nc.tensor.transpose(pt[:, i * P:(i + 1) * P], src[:, slot_i, :], ident[:])
             if which == 0:
                 nc.vector.tensor_copy(out=dst[:, 1024 * half:1024 * (half + 1)], in_=pt[:])
             else:
@@ -119,8 +126,8 @@ def tile_slidingwindowattention_kernel(tc, q, k, v, out):
             vset = vsets[h % 2]
             vg = vpool.tile([P, NB, D, 4], BF16, tag="vg", align_bytes=64)
             nc.vector.tensor_copy(
-                out=vg[:].rearrange("p b (c i) t -> p b c t i", i=4),
-                in_=vr[:].rearrange("p (b t) (c i) -> p b c t i", t=4, i=4))
+                out=vg[:].rearrange("p b d (u e) -> p b d u e", e=2),
+                in_=vr[:].rearrange("p (b e u) d -> p b d u e", e=2, u=2))
             nc.vector.quantize_mx(
                 out=vset["vq"][:].rearrange("p b d -> p (b d)").bitcast(FP8X4),
                 scales=vset["vs"][:].rearrange("p b d -> p (b d)"),
@@ -142,13 +149,13 @@ def tile_slidingwindowattention_kernel(tc, q, k, v, out):
 
         def s_lead(h, j):
             hd = heads[h]
-            kTv = hd["kT"][:].rearrange("d (b t c) -> d b t c", t=4, c=P)
-            sl = ps_l.tile([P, TPB, 4, Q], F32, tag="sl")
+            kTv = hd["kT"][:].rearrange("d (b u x) -> d b u x", u=2, x=2 * P)
+            sl = ps_l.tile([P, TPB, 2, 2 * Q], F32, tag="sl")
             for r in range(TPB):
                 i = TPB * j + r
-                nc.tensor.matmul(sl[:, r, :, :], lhsT=hd["qT"][:, i * P:(i + 1) * P], rhs=kTv[:, j - 1, :, Q * r:Q * (r + 1)], start=True, stop=False)
+                nc.tensor.matmul(sl[:, r, :, :], lhsT=hd["qT"][:, i * P:(i + 1) * P], rhs=kTv[:, j - 1, :, 2 * Q * r:2 * Q * (r + 1)], start=True, stop=False)
                 nc.tensor.matmul(sl[:, r, :, :], lhsT=ident[:], rhs=mask[:, 1, :, :], start=False, stop=True)
-            zl = zlpool.tile([P, TPB, 4, Q], F32, tag="zl")
+            zl = zlpool.tile([P, TPB, 2, 2 * Q], F32, tag="zl")
             nbl = small.tile([P, TPB], F32, tag="nbl")
             for r in range(TPB):
                 nc.vector.tensor_scalar(
@@ -156,7 +163,7 @@ def tile_slidingwindowattention_kernel(tc, q, k, v, out):
                     op0=ALU.mult, op1=ALU.min, accum_out=nbl[:, r:r + 1])
             st[("zl", h, j)] = zl
             st[("nbl", h, j)] = nbl
-            st[("el", h, j)] = elpool.tile([P, 4, P], BF16, tag="el", name="el")
+            st[("el", h, j)] = elpool.tile([P, 2, 2 * P], BF16, tag="el", name="el")
 
         def s_win(x):
             h, j, r = tiles[x]
@@ -165,25 +172,25 @@ def tile_slidingwindowattention_kernel(tc, q, k, v, out):
                 st[("den", h, j)] = small.tile([P, TPB, 2], F32, tag="den", name="den")
                 if j > 0:
                     s_lead(h, j)
-            kTv = hd["kT"][:].rearrange("d (b t c) -> d b t c", t=4, c=P)
+            kTv = hd["kT"][:].rearrange("d (b u x) -> d b u x", u=2, x=2 * P)
             i = TPB * j + r
             qcols = hd["qT"][:, i * P:(i + 1) * P]
-            cut = Q * (r + 1)
-            sw = ps_w.tile([P, 4, P], F32, tag="sw")
+            cut = 2 * Q * (r + 1)
+            sw = ps_w.tile([P, 2, 2 * P], F32, tag="sw")
             nc.tensor.matmul(sw[:, :, 0:cut], lhsT=qcols, rhs=kTv[:, j, :, 0:cut], start=True, stop=False)
-            if j > 0 and cut < P:
-                nc.tensor.matmul(sw[:, :, cut:P], lhsT=qcols, rhs=kTv[:, j - 1, :, cut:P], start=False, stop=False)
-            nc.tensor.matmul(sw[:, :, cut - Q:cut], lhsT=ident[:], rhs=mask[:, 0, :, :], start=False, stop=True)
+            if j > 0 and cut < 2 * P:
+                nc.tensor.matmul(sw[:, :, cut:2 * P], lhsT=qcols, rhs=kTv[:, j - 1, :, cut:2 * P], start=False, stop=False)
+            nc.tensor.matmul(sw[:, :, cut - 2 * Q:cut], lhsT=ident[:], rhs=mask[:, 0, :, :], start=False, stop=True)
             st[("sw", x)] = sw
 
         def seen(x):
             h, j, r = tiles[x]
-            return P if j > 0 else Q * (r + 1)
+            return 2 * P if j > 0 else 2 * Q * (r + 1)
 
         def row_max(x):
             h, j, r = tiles[x]
             sw = st[("sw", x)]
-            zw = zpool.tile([P, 4, P], F32, tag="zw")
+            zw = zpool.tile([P, 2, 2 * P], F32, tag="zw")
             nb = small.tile([P, 1], F32, tag="nb")
             nc.vector.tensor_scalar(
                 out=zw[:, :, 0:seen(x)], in0=sw[:, :, 0:seen(x)], scalar1=-SCALE,
@@ -201,20 +208,21 @@ def tile_slidingwindowattention_kernel(tc, q, k, v, out):
             nc.scalar.activation(out=ew[:, :, 0:seen(x)], in_=zw[:, :, 0:seen(x)], func=ACTF.Exp, bias=nb[:], scale=-1.0, accum_out=den[:, r, 0:1])
             if j > 0:
                 nc.scalar.activation(
-                    out=st[("el", h, j)][:, :, Q * r:Q * (r + 1)], in_=st[("zl", h, j)][:, r, :, :],
+                    out=st[("el", h, j)][:, :, 2 * Q * r:2 * Q * (r + 1)], in_=st[("zl", h, j)][:, r, :, :],
                     func=ACTF.Exp, bias=nb[:], scale=-1.0, accum_out=den[:, r, 1:2])
 
         def flip(key, src):
-            et = ps_m.tile([P, 4, P], BF16, tag="misc", name="et")
-            for t in range(4):
-                nc.tensor.transpose(et[:, t, :], src[:, t, :], ident[:])
+            et = ps_m.tile([P, 2, P], F32, tag="misc", name="et")
+            words = src[:].rearrange("p u x -> p (u x)").bitcast(F32)
+            for u in range(2):
+                nc.tensor.transpose(et[:, u, :], words[:, u * P:(u + 1) * P], ident_f[:])
             st[("et",) + key] = et
 
         def evict(key, on_scalar):
             et = st[("et",) + key]
             g = gpool.tile([P, P, 4], BF16, tag="g", align_bytes=64)
-            dst = g[:].rearrange("p (c i) t -> p c t i", i=4)
-            src = et[:].rearrange("p t (c i) -> p c t i", i=4)
+            dst = g[:].rearrange("p n t -> p (n t)").bitcast(F32).rearrange("p (n u) -> p n u", u=2)
+            src = et[:].rearrange("p u n -> p n u")
             if on_scalar:
                 nc.scalar.copy(out=dst, in_=src)
             else:

@@ -22,7 +22,7 @@ NB = N // W
 TPB = W // P
 Q = P // TPB
 SCALE = 0.125
-NEG = -(2.0 ** 100)
+BIG = 2.0 ** 100
 FLOPS = 2 * 2 * H * (2 * NB - 1) * W * W * D
 MANUAL = False
 N_EW = 4
@@ -41,9 +41,8 @@ def tile_slidingwindowattention_kernel(tc, q, k, v, out):
         small = ctx.enter_context(tc.tile_pool(name="small", bufs=6))
         opool = ctx.enter_context(tc.tile_pool(name="opool", bufs=3))
         zpool = ctx.enter_context(tc.tile_pool(name="zpool", bufs=6))
-        zlpool = ctx.enter_context(tc.tile_pool(name="zlpool", bufs=3))
-        ps_w = ctx.enter_context(tc.psum_pool(name="ps_w", bufs=3))
-        ps_l = ctx.enter_context(tc.psum_pool(name="ps_l", bufs=1))
+        ps_w = ctx.enter_context(tc.psum_pool(name="ps_w", bufs=2))
+        ps_l = ctx.enter_context(tc.psum_pool(name="ps_l", bufs=2))
         ps_m = ctx.enter_context(tc.psum_pool(name="ps_m", bufs=4))
 
         def zero(t, pattern):
@@ -56,11 +55,11 @@ def tile_slidingwindowattention_kernel(tc, q, k, v, out):
         mask_f = const.tile([P, 2, P], F32)
         nc.gpsimd.memset(mask_f[:], 0.0)
         nc.gpsimd.affine_select(
-            out=mask_f[:, 0, :], in_=mask_f[:, 0, :], compare_op=ALU.is_ge, fill=NEG,
+            out=mask_f[:, 0, :], in_=mask_f[:, 0, :], compare_op=ALU.is_ge, fill=BIG,
             base=0, pattern=[[-1, 2], [-4, Q], [-2, 2]], channel_multiplier=1,
         )
         nc.gpsimd.affine_select(
-            out=mask_f[:, 1, :], in_=mask_f[:, 1, :], compare_op=ALU.is_ge, fill=NEG,
+            out=mask_f[:, 1, :], in_=mask_f[:, 1, :], compare_op=ALU.is_ge, fill=BIG,
             base=-1, pattern=[[1, 2], [4, Q], [2, 2]], channel_multiplier=-1,
         )
         mask = const.tile([P, 2, 2, 2 * Q], BF16)
@@ -117,7 +116,7 @@ def tile_slidingwindowattention_kernel(tc, q, k, v, out):
                     slot_i = 8 * half + 2 * (2 * b_loc + hh) + u
                 nc.tensor.transpose(pt[:, i * P:(i + 1) * P], src[:, slot_i, :], ident[:])
             if which == 0:
-                nc.vector.tensor_copy(out=dst[:, 1024 * half:1024 * (half + 1)], in_=pt[:])
+                nc.vector.tensor_scalar(out=dst[:, 1024 * half:1024 * (half + 1)], in0=pt[:], scalar1=-SCALE, scalar2=None, op0=ALU.mult)
             else:
                 nc.scalar.copy(out=dst[:, 1024 * half:1024 * (half + 1)], in_=pt[:])
 
@@ -155,13 +154,9 @@ def tile_slidingwindowattention_kernel(tc, q, k, v, out):
                 i = TPB * j + r
                 nc.tensor.matmul(sl[:, r, :, :], lhsT=hd["qT"][:, i * P:(i + 1) * P], rhs=kTv[:, j - 1, :, 2 * Q * r:2 * Q * (r + 1)], start=True, stop=False)
                 nc.tensor.matmul(sl[:, r, :, :], lhsT=ident[:], rhs=mask[:, 1, :, :], start=False, stop=True)
-            zl = zlpool.tile([P, TPB, 2, 2 * Q], F32, tag="zl")
             nbl = small.tile([P, TPB], F32, tag="nbl")
-            for r in range(TPB):
-                nc.vector.tensor_scalar(
-                    out=zl[:, r, :, :], in0=sl[:, r, :, :], scalar1=-SCALE, scalar2=None,
-                    op0=ALU.mult, op1=ALU.min, accum_out=nbl[:, r:r + 1])
-            st[("zl", h, j)] = zl
+            nc.vector.tensor_reduce(out=nbl[:], in_=sl[:].rearrange("p r u x -> p r (u x)"), axis=AX.X, op=ALU.min)
+            st[("zl", h, j)] = sl
             st[("nbl", h, j)] = nbl
             st[("el", h, j)] = elpool.tile([P, 2, 2 * P], BF16, tag="el", name="el")
 
@@ -193,7 +188,7 @@ def tile_slidingwindowattention_kernel(tc, q, k, v, out):
             zw = zpool.tile([P, 2, 2 * P], F32, tag="zw")
             nb = small.tile([P, 1], F32, tag="nb")
             nc.vector.tensor_scalar(
-                out=zw[:, :, 0:seen(x)], in0=sw[:, :, 0:seen(x)], scalar1=-SCALE,
+                out=zw[:, :, 0:seen(x)], in0=sw[:, :, 0:seen(x)], scalar1=1.0,
                 scalar2=st[("nbl", h, j)][:, r:r + 1] if j > 0 else None,
                 op0=ALU.mult, op1=ALU.min, accum_out=nb[:])
             st[("zw", x)] = zw

@@ -37,7 +37,7 @@ def tile_slidingwindowattention_kernel(tc, q, k, v, out):
         vpool = ctx.enter_context(tc.tile_pool(name="vpool", bufs=2))
         elpool = ctx.enter_context(tc.tile_pool(name="elpool", bufs=2))
         gpool = ctx.enter_context(tc.tile_pool(name="gpool", bufs=4))
-        cpool = ctx.enter_context(tc.tile_pool(name="cpool", bufs=12))
+        cpool = ctx.enter_context(tc.tile_pool(name="cpool", bufs=6))
         small = ctx.enter_context(tc.tile_pool(name="small", bufs=6))
         opool = ctx.enter_context(tc.tile_pool(name="opool", bufs=3))
         zpool = ctx.enter_context(tc.tile_pool(name="zpool", bufs=6))
@@ -206,42 +206,44 @@ def tile_slidingwindowattention_kernel(tc, q, k, v, out):
                     out=st[("el", h, j)][:, :, 2 * Q * r:2 * Q * (r + 1)], in_=st[("zl", h, j)][:, r, :, :],
                     func=ACTF.Exp, bias=nb[:], scale=-1.0, accum_out=den[:, r, 1:2])
 
-        def flip(key, src):
-            et = ps_m.tile([P, 2, P], F32, tag="misc", name="et")
+        def flip(key, part, parts, src):
+            if part == 0:
+                st[("et",) + key] = ps_m.tile([P, parts, 2, P], F32, tag="misc", name="et")
+            et = st[("et",) + key]
             words = src[:].rearrange("p u x -> p (u x)").bitcast(F32)
             for u in range(2):
-                nc.tensor.transpose(et[:, u, :], words[:, u * P:(u + 1) * P], ident_f[:])
-            st[("et",) + key] = et
+                nc.tensor.transpose(et[:, part, u, :], words[:, u * P:(u + 1) * P], ident_f[:])
 
-        def evict(key, on_scalar):
+        def evict(key, parts, on_scalar):
             et = st[("et",) + key]
-            g = gpool.tile([P, P, 4], BF16, tag="g", align_bytes=64)
-            dst = g[:].rearrange("p n t -> p (n t)").bitcast(F32).rearrange("p (n u) -> p n u", u=2)
-            src = et[:].rearrange("p u n -> p n u")
+            g = gpool.tile([P, parts, P, 4], BF16, tag="g%d" % parts, align_bytes=64)
+            dst = g[:].rearrange("p a n t -> p (a n t)").bitcast(F32).rearrange("p (a n u) -> p a n u", a=parts, u=2)
+            src = et[:].rearrange("p a u n -> p a n u")
             if on_scalar:
                 nc.scalar.copy(out=dst, in_=src)
             else:
                 nc.vector.tensor_copy(out=dst, in_=src)
             st[("g",) + key] = g
 
-        def quant(key):
+        def quant(key, parts):
             g = st[("g",) + key]
-            codes = cpool.tile([P, P], U32, tag="codes", align_bytes=64)
-            scl = cpool.tile([P, P], U8, tag="scl", align_bytes=64)
-            nc.vector.quantize_mx(out=codes[:].bitcast(FP8X4), scales=scl[:], in_=g[:].rearrange("p n t -> p (n t)"))
+            codes = cpool.tile([P, parts * P], U32, tag="codes%d" % parts, align_bytes=64)
+            scl = cpool.tile([P, parts * P], U8, tag="scl%d" % parts, align_bytes=64)
+            nc.vector.quantize_mx(out=codes[:].bitcast(FP8X4), scales=scl[:], in_=g[:].rearrange("p a n t -> p (a n t)"))
             st[("c",) + key] = (codes, scl)
 
         def mx(h, j):
             vset = vsets[h % 2]
             acc = ps_m.tile([P, TPB, D], F32, tag="misc", name="acc")
             for r in range(TPB):
-                codes, scl = st[("c", "w", h, j, r)]
+                codes, scl = st[("c", "w", h, j, r // 2)]
+                cols = slice((r % 2) * P, (r % 2 + 1) * P)
                 if r < TPB - 1:
                     rhs, rsc = vset["vwc"][:, r, j, :], vset["vws"][:, r, j, :]
                 else:
                     rhs, rsc = vset["vq"][:, j, :], vset["vs"][:, j, :]
                 nc.tensor.matmul_mx(
-                    out=acc[:, r, :], lhsT=codes[:].bitcast(FP8X4), lhsT_scale=scl[:],
+                    out=acc[:, r, :], lhsT=codes[:, cols].bitcast(FP8X4), lhsT_scale=scl[:, cols],
                     rhs=rhs.bitcast(FP8X4), rhs_scale=rsc,
                     start=(r == 0), stop=(j == 0 and r == TPB - 1))
             if j > 0:
@@ -274,15 +276,17 @@ def tile_slidingwindowattention_kernel(tc, q, k, v, out):
             x = s - 3
             if ok(x):
                 h, j, r = tiles[x]
-                evict(("w", h, j, r), r < TPB - 1 or j % 2 == 0)
+                if r % 2 == 1:
+                    evict(("w", h, j, r // 2), 2, True)
                 if r == TPB - 1 and j > 0:
-                    evict(("l", h, j), j % 2 == 1)
+                    evict(("l", h, j), 1, True)
             x = s - 4
             if ok(x):
                 h, j, r = tiles[x]
-                quant(("w", h, j, r))
+                if r % 2 == 1:
+                    quant(("w", h, j, r // 2), 2)
                 if r == TPB - 1 and j > 0:
-                    quant(("l", h, j))
+                    quant(("l", h, j), 1)
             if ok(s + 1):
                 s_win(s + 1)
             if ok(s):
@@ -292,9 +296,9 @@ def tile_slidingwindowattention_kernel(tc, q, k, v, out):
             x = s - 2
             if ok(x):
                 h, j, r = tiles[x]
-                flip(("w", h, j, r), ew_tiles[x % N_EW])
+                flip(("w", h, j, r // 2), r % 2, 2, ew_tiles[x % N_EW])
                 if r == TPB - 1 and j > 0:
-                    flip(("l", h, j), st[("el", h, j)])
+                    flip(("l", h, j), 0, 1, st[("el", h, j)])
             x = s - 4
             if ok(x) and tiles[x][2] == TPB - 1:
                 mx(tiles[x][0], tiles[x][1])

@@ -12,6 +12,7 @@ U8 = mybir.dt.uint8
 ALU = mybir.AluOpType
 ACTF = mybir.ActivationFunctionType
 AX = mybir.AxisListType
+ET = mybir.EngineType
 
 H = 8
 N = 2048
@@ -20,11 +21,11 @@ W = 512
 P = 128
 NB = N // W
 TPB = W // P
+TPH = N // P
 Q = P // TPB
 SCALE = 0.125
 BIG = 2.0 ** 100
 FLOPS = 2 * 2 * H * (2 * NB - 1) * W * W * D
-MANUAL = False
 N_EW = 4
 
 
@@ -35,23 +36,23 @@ def tile_slidingwindowattention_kernel(tc, q, k, v, out):
         raw = ctx.enter_context(tc.tile_pool(name="raw", bufs=3))
         tpose = ctx.enter_context(tc.tile_pool(name="tpose", bufs=2))
         vpool = ctx.enter_context(tc.tile_pool(name="vpool", bufs=2))
-        elpool = ctx.enter_context(tc.tile_pool(name="elpool", bufs=2))
+        elpool = ctx.enter_context(tc.tile_pool(name="elpool", bufs=3))
         gpool = ctx.enter_context(tc.tile_pool(name="gpool", bufs=4))
         cpool = ctx.enter_context(tc.tile_pool(name="cpool", bufs=6))
-        small = ctx.enter_context(tc.tile_pool(name="small", bufs=6))
+        small = ctx.enter_context(tc.tile_pool(name="small", bufs=8))
         opool = ctx.enter_context(tc.tile_pool(name="opool", bufs=3))
-        zpool = ctx.enter_context(tc.tile_pool(name="zpool", bufs=6))
-        ps_w = ctx.enter_context(tc.psum_pool(name="ps_w", bufs=2))
-        ps_l = ctx.enter_context(tc.psum_pool(name="ps_l", bufs=2))
-        ps_m = ctx.enter_context(tc.psum_pool(name="ps_m", bufs=4))
+        psum = ctx.enter_context(tc.psum_pool(name="psum", bufs=1))
+        ctx.enter_context(tc.manual_schedule(engines={ET.PE, ET.Activation, ET.DVE, ET.Pool}))
 
-        def zero(t, pattern):
-            nc.vector.memset(t[:].rearrange(pattern).bitcast(I32), 0)
+        def zero(ap):
+            nc.vector.memset(ap.bitcast(I32), 0)
+
+        dummy = const.tile([P, 2], F32)
+        nc.vector.memset(dummy[:], 0.0)
+        nc.scalar.activation(out=dummy[:, 1:2], in_=dummy[:, 0:1], func=ACTF.Exp)
 
         ident = const.tile([P, P], BF16)
         make_identity(nc, ident[:])
-        ident_f = const.tile([P, P], F32)
-        make_identity(nc, ident_f[:])
         mask_f = const.tile([P, 2, P], F32)
         nc.gpsimd.memset(mask_f[:], 0.0)
         nc.gpsimd.affine_select(
@@ -62,16 +63,54 @@ def tile_slidingwindowattention_kernel(tc, q, k, v, out):
             out=mask_f[:, 1, :], in_=mask_f[:, 1, :], compare_op=ALU.is_ge, fill=BIG,
             base=-1, pattern=[[1, 2], [4, Q], [2, 2]], channel_multiplier=-1,
         )
-        mask = const.tile([P, 2, 2, 2 * Q], BF16)
-        nc.vector.tensor_copy(out=mask[:].rearrange("p m u x -> p m (u x)"), in_=mask_f[:])
+        ident_f = const.tile([P, P], F32)
+        make_identity(nc, ident_f[:])
 
-        ew_tiles = []
-        for i in range(N_EW):
-            ew0 = const.tile([P, 2, 2 * P], BF16, name="ew%d" % i)
-            zero(ew0, "p u x -> p (u x)")
-            ew_tiles.append(ew0)
+        heads = {}
+        st = {}
+
+        def load_raw(h):
+            hd = {
+                "qr": raw.tile([P, N // P, D], BF16, tag="qr", name="qr"),
+                "kr": raw.tile([P, N // P, D], BF16, tag="kr", name="kr"),
+                "vr": raw.tile([P, N // P, D], BF16, tag="vr", name="vr"),
+            }
+            heads[h] = hd
+
+        def load_q(h, t0, t1):
+            rows = q[0, h].rearrange("(g p) d -> p g d", p=P)
+            nc.sync.dma_start(out=heads[h]["qr"][:, t0:t1, :], in_=rows[:, t0:t1, :])
+
+        def load_k(h, t0, t1):
+            rows = k[0, h].rearrange("(g p s) d -> p g (s d)", p=P, s=2)
+            dst = heads[h]["kr"][:].rearrange("p (g s) d -> p g (s d)", s=2)
+            nc.sync.dma_start(out=dst[:, t0 // 2:t1 // 2, :], in_=rows[:, t0 // 2:t1 // 2, :])
+
+        def load_v(h):
+            rows = v[0, h].rearrange("(b p t) d -> p b (t d)", p=P, t=4)
+            nc.sync.dma_start(out=heads[h]["vr"][:].rearrange("p (b t) d -> p b (t d)", t=4), in_=rows)
+
+        def load(h):
+            load_raw(h)
+            load_v(h)
+            load_q(h, 0, 8)
+            load_k(h, 0, 8)
+            load_q(h, 8, 16)
+            load_k(h, 8, 16)
+
+        load_raw(0)
+        load_q(0, 0, 4)
+        load_k(0, 0, 4)
+        load_q(0, 4, 8)
+        load_k(0, 4, 8)
+        load_v(0)
+        load_q(0, 8, 16)
+        load_k(0, 8, 16)
+        load(1)
+
         vsets = []
-        for i in range(2):
+
+        def make_vset(i):
             vset = {
                 "vq": const.tile([P, NB, D], U32, name="vq%d" % i, align_bytes=64),
                 "vs": const.tile([P, NB, D], U8, name="vs%d" % i, align_bytes=64),
@@ -80,58 +119,66 @@ def tile_slidingwindowattention_kernel(tc, q, k, v, out):
                 "vbc": const.tile([P, NB - 1, TPB, D], U32, name="vbc%d" % i, align_bytes=64),
                 "vbs": const.tile([P, NB - 1, TPB, D], U8, name="vbs%d" % i, align_bytes=64),
             }
-            zero(vset["vs"], "p b d -> p (b d)")
-            for nm in ("vwc", "vws", "vbc", "vbs"):
-                zero(vset[nm], "p a b d -> p (a b d)")
+            zero(vset["vs"][:].rearrange("p b d -> p (b d)"))
+            zero(vset["vwc"][:, :, 0, :])
+            zero(vset["vws"][:, :, 0, :])
+            zero(vset["vbc"][:].rearrange("p a b d -> p (a b d)"))
+            zero(vset["vbs"][:].rearrange("p a b d -> p (a b d)"))
             vsets.append(vset)
 
-        heads = {}
+        make_vset(0)
+        mask = const.tile([P, 2, 2, 2 * Q], BF16)
+        nc.vector.tensor_copy(out=mask[:].rearrange("p m u x -> p m (u x)"), in_=mask_f[:])
+        ew_tiles = []
+        for i in range(N_EW):
+            ew0 = const.tile([P, 2, 2 * P], BF16, name="ew%d" % i)
+            zero(ew0[:].rearrange("p u x -> p (u x)"))
+            ew_tiles.append(ew0)
 
-        def load(h):
-            qr = raw.tile([P, N // P, D], BF16, tag="qr")
-            kr = raw.tile([P, N // P, D], BF16, tag="kr")
-            vr = raw.tile([P, N // P, D], BF16, tag="vr")
-            q_rows = q[0, h].rearrange("(g p) d -> p g d", p=P)
-            k_rows = k[0, h].rearrange("(g p s) d -> p g (s d)", p=P, s=2)
-            v_rows = v[0, h].rearrange("(b p t) d -> p b (t d)", p=P, t=4)
-            kr2 = kr[:].rearrange("p (g s) d -> p g (s d)", s=2)
-            nc.sync.dma_start(out=qr[:, 0:8, :], in_=q_rows[:, 0:8, :])
-            nc.sync.dma_start(out=kr2[:, 0:4, :], in_=k_rows[:, 0:4, :])
-            nc.sync.dma_start(out=vr[:].rearrange("p (b t) d -> p b (t d)", t=4), in_=v_rows)
-            nc.sync.dma_start(out=qr[:, 8:16, :], in_=q_rows[:, 8:16, :])
-            nc.sync.dma_start(out=kr2[:, 4:8, :], in_=k_rows[:, 4:8, :])
-            heads[h] = {"qr": qr, "kr": kr, "vr": vr}
-
-        def prep_qk(h, which, half):
+        def prep_pe(h, which, t0, n, bank):
             src = heads[h]["qr" if which == 0 else "kr"]
-            if half == 0:
-                heads[h]["qT" if which == 0 else "kT"] = tpose.tile([P, N], BF16, tag="qT" if which == 0 else "kT", name="xT")
-            dst = heads[h]["qT" if which == 0 else "kT"]
-            pt = ps_m.tile([P, 8 * P], BF16, tag="misc")
-            for i in range(8):
-                if which == 0:
-                    slot_i = 8 * half + i
-                else:
-                    b_loc, u, hh = i // 4, (i // 2) % 2, i % 2
-                    slot_i = 8 * half + 2 * (2 * b_loc + hh) + u
-                nc.tensor.transpose(pt[:, i * P:(i + 1) * P], src[:, slot_i, :], ident[:])
-            if which == 0:
-                nc.vector.tensor_scalar(out=dst[:, 1024 * half:1024 * (half + 1)], in0=pt[:], scalar1=-SCALE, scalar2=None, op0=ALU.mult)
-            else:
-                nc.scalar.copy(out=dst[:, 1024 * half:1024 * (half + 1)], in_=pt[:])
+            pt = psum.tile([P, 8 * P], BF16, tag=bank, name="pt")
+            for i in range(n):
+                t = t0 + i
+                if which == 1:
+                    b, u, hh = t // 4, (t // 2) % 2, t % 2
+                    t = 4 * b + 2 * hh + u
+                nc.tensor.transpose(pt[:, i * P:(i + 1) * P], src[:, t, :], ident[:])
+            st[("pt", h, which, t0)] = pt
 
-        def prep_v(h):
-            vr = heads[h]["vr"]
+        def prep_copy(h, which, t0, n):
+            nm = "qT" if which == 0 else "kT"
+            if t0 == 0:
+                heads[h][nm] = tpose.tile([P, N], BF16, tag=nm, name=nm)
+            dst = heads[h][nm][:, P * t0:P * (t0 + n)]
+            pt = st[("pt", h, which, t0)]
+            if which == 0:
+                nc.vector.tensor_scalar(out=dst, in0=pt[:, 0:n * P], scalar1=-SCALE, scalar2=None, op0=ALU.mult)
+            else:
+                nc.scalar.copy(out=dst, in_=pt[:, 0:n * P])
+
+        def regroup(h, engine, b0, b1, d0, d1):
+            if "vg" not in heads[h]:
+                heads[h]["vg"] = vpool.tile([P, NB, D, 4], BF16, tag="vg", name="vg", align_bytes=64)
+            dst = heads[h]["vg"][:].rearrange("p b d (u e) -> p b d u e", e=2)
+            src = heads[h]["vr"][:].rearrange("p (b e u) d -> p b d u e", e=2, u=2)
+            for b in range(b0, b1):
+                if engine == "vector":
+                    nc.vector.tensor_copy(out=dst[:, b, d0:d1], in_=src[:, b, d0:d1])
+                else:
+                    nc.gpsimd.tensor_scalar(out=dst[:, b, d0:d1], in0=src[:, b, d0:d1], scalar1=1.0, scalar2=0.0, op0=ALU.mult, op1=ALU.add)
+
+        def quant_v(h, b0, b1):
             vset = vsets[h % 2]
-            vg = vpool.tile([P, NB, D, 4], BF16, tag="vg", align_bytes=64)
-            nc.vector.tensor_copy(
-                out=vg[:].rearrange("p b d (u e) -> p b d u e", e=2),
-                in_=vr[:].rearrange("p (b e u) d -> p b d u e", e=2, u=2))
+            vg = heads[h]["vg"]
             nc.vector.quantize_mx(
-                out=vset["vq"][:].rearrange("p b d -> p (b d)").bitcast(FP8X4),
-                scales=vset["vs"][:].rearrange("p b d -> p (b d)"),
-                in_=vg[:].rearrange("p b d t -> p (b d t)"),
+                out=vset["vq"][:, b0:b1, :].rearrange("p b d -> p (b d)").bitcast(FP8X4),
+                scales=vset["vs"][:, b0:b1, :].rearrange("p b d -> p (b d)"),
+                in_=vg[:, b0:b1, :, :].rearrange("p b d t -> p (b d t)"),
             )
+
+        def spread_v(h):
+            vset = vsets[h % 2]
             for src_n, win_n, bd_n in (("vq", "vwc", "vbc"), ("vs", "vws", "vbs")):
                 src = vset[src_n][:].bitcast(I32)
                 win = vset[win_n][:].bitcast(I32)
@@ -144,37 +191,35 @@ def tile_slidingwindowattention_kernel(tc, q, k, v, out):
                     nc.sync.dma_start(out=bd[Q * s:Q * (s + 1), :, s, :], in_=src[Q * s:Q * (s + 1), 0:NB - 1, :])
 
         tiles = [(h, j, r) for h in range(H) for j in range(NB) for r in range(TPB)]
-        st = {}
+        blocks = [(h, j) for h in range(H) for j in range(NB)]
 
-        def s_lead(h, j):
+        def kT_view(h):
+            return heads[h]["kT"][:].rearrange("d (b u x) -> d b u x", u=2, x=2 * P)
+
+        def lead_scores(bk):
+            h, j = blocks[bk]
             hd = heads[h]
-            kTv = hd["kT"][:].rearrange("d (b u x) -> d b u x", u=2, x=2 * P)
-            sl = ps_l.tile([P, TPB, 2, 2 * Q], F32, tag="sl")
+            sl = psum.tile([P, TPB, 2, 2 * Q], F32, tag="sl%d" % (bk % 2), name="sl")
             for r in range(TPB):
                 i = TPB * j + r
-                nc.tensor.matmul(sl[:, r, :, :], lhsT=hd["qT"][:, i * P:(i + 1) * P], rhs=kTv[:, j - 1, :, 2 * Q * r:2 * Q * (r + 1)], start=True, stop=False)
+                nc.tensor.matmul(sl[:, r, :, :], lhsT=hd["qT"][:, i * P:(i + 1) * P], rhs=kT_view(h)[:, j - 1, :, 2 * Q * r:2 * Q * (r + 1)], start=True, stop=False)
                 nc.tensor.matmul(sl[:, r, :, :], lhsT=ident[:], rhs=mask[:, 1, :, :], start=False, stop=True)
-            nbl = small.tile([P, TPB], F32, tag="nbl")
-            nc.vector.tensor_reduce(out=nbl[:], in_=sl[:].rearrange("p r u x -> p r (u x)"), axis=AX.X, op=ALU.min)
-            st[("zl", h, j)] = sl
-            st[("nbl", h, j)] = nbl
-            st[("el", h, j)] = elpool.tile([P, 2, 2 * P], BF16, tag="el", name="el")
+            st[("sl", bk)] = sl
 
-        def s_win(x):
+        def lead_min(bk):
+            nbl = small.tile([P, TPB], F32, tag="nbl")
+            nc.vector.tensor_reduce(out=nbl[:], in_=st[("sl", bk)][:].rearrange("p r u x -> p r (u x)"), axis=AX.X, op=ALU.min)
+            st[("nbl", bk)] = nbl
+
+        def scores(x):
             h, j, r = tiles[x]
-            hd = heads[h]
-            if r == 0:
-                st[("den", h, j)] = small.tile([P, TPB, 2], F32, tag="den", name="den")
-                if j > 0:
-                    s_lead(h, j)
-            kTv = hd["kT"][:].rearrange("d (b u x) -> d b u x", u=2, x=2 * P)
             i = TPB * j + r
-            qcols = hd["qT"][:, i * P:(i + 1) * P]
+            qcols = heads[h]["qT"][:, i * P:(i + 1) * P]
             cut = 2 * Q * (r + 1)
-            sw = ps_w.tile([P, 2, 2 * P], F32, tag="sw")
-            nc.tensor.matmul(sw[:, :, 0:cut], lhsT=qcols, rhs=kTv[:, j, :, 0:cut], start=True, stop=False)
+            sw = psum.tile([P, 2, 2 * P], F32, tag="sw%d" % (x % 3), name="sw")
+            nc.tensor.matmul(sw[:, :, 0:cut], lhsT=qcols, rhs=kT_view(h)[:, j, :, 0:cut], start=True, stop=False)
             if j > 0 and cut < 2 * P:
-                nc.tensor.matmul(sw[:, :, cut:2 * P], lhsT=qcols, rhs=kTv[:, j - 1, :, cut:2 * P], start=False, stop=False)
+                nc.tensor.matmul(sw[:, :, cut:2 * P], lhsT=qcols, rhs=kT_view(h)[:, j - 1, :, cut:2 * P], start=False, stop=False)
             nc.tensor.matmul(sw[:, :, cut - 2 * Q:cut], lhsT=ident[:], rhs=mask[:, 0, :, :], start=False, stop=True)
             st[("sw", x)] = sw
 
@@ -182,61 +227,64 @@ def tile_slidingwindowattention_kernel(tc, q, k, v, out):
             h, j, r = tiles[x]
             return 2 * P if j > 0 else 2 * Q * (r + 1)
 
-        def row_max(x):
-            h, j, r = tiles[x]
+        def window_min(x):
+            nbw = small.tile([P, 1], F32, tag="nbw")
             sw = st[("sw", x)]
-            zw = zpool.tile([P, 2, 2 * P], F32, tag="zw")
-            nb = small.tile([P, 1], F32, tag="nb")
-            nc.vector.tensor_scalar(
-                out=zw[:, :, 0:seen(x)], in0=sw[:, :, 0:seen(x)], scalar1=1.0,
-                scalar2=st[("nbl", h, j)][:, r:r + 1] if j > 0 else None,
-                op0=ALU.mult, op1=ALU.min, accum_out=nb[:])
-            st[("zw", x)] = zw
-            st[("nb", x)] = nb
+            if seen(x) == 2 * P:
+                nc.vector.tensor_reduce(out=nbw[:], in_=sw[:].rearrange("p u x -> p (u x)"), axis=AX.X, op=ALU.min)
+            else:
+                nc.vector.tensor_reduce(out=nbw[:], in_=sw[:, :, 0:seen(x)], axis=AX.XY, op=ALU.min)
+            st[("nb", x)] = nbw
+
+        def join(x):
+            h, j, r = tiles[x]
+            if j > 0:
+                nb = small.tile([P, 1], F32, tag="nb")
+                nc.gpsimd.tensor_scalar(out=nb[:], in0=st[("nb", x)][:], scalar1=st[("nbl", x // TPB)][:, r:r + 1], scalar2=None, op0=ALU.min)
+                st[("nb", x)] = nb
 
         def expo(x):
             h, j, r = tiles[x]
-            zw = st[("zw", x)]
+            bk = x // TPB
             nb = st[("nb", x)]
-            den = st[("den", h, j)]
-            ew = ew_tiles[x % N_EW]
-            nc.scalar.activation(out=ew[:, :, 0:seen(x)], in_=zw[:, :, 0:seen(x)], func=ACTF.Exp, bias=nb[:], scale=-1.0, accum_out=den[:, r, 0:1])
+            if r == 0:
+                st[("den", bk)] = small.tile([P, TPB, 2], F32, tag="den", name="den")
+                if j > 0:
+                    st[("el", bk)] = elpool.tile([P, 2, 2 * P], BF16, tag="el", name="el")
+            den = st[("den", bk)]
+            nc.scalar.activation(out=ew_tiles[x % N_EW][:, :, 0:seen(x)], in_=st[("sw", x)][:, :, 0:seen(x)], func=ACTF.Exp, bias=nb[:], scale=-1.0, accum_out=den[:, r, 0:1])
             if j > 0:
                 nc.scalar.activation(
-                    out=st[("el", h, j)][:, :, 2 * Q * r:2 * Q * (r + 1)], in_=st[("zl", h, j)][:, r, :, :],
+                    out=st[("el", bk)][:, :, 2 * Q * r:2 * Q * (r + 1)], in_=st[("sl", bk)][:, r, :, :],
                     func=ACTF.Exp, bias=nb[:], scale=-1.0, accum_out=den[:, r, 1:2])
 
-        def flip(key, part, parts, src):
-            if part == 0:
-                st[("et",) + key] = ps_m.tile([P, parts, 2, P], F32, tag="misc", name="et")
-            et = st[("et",) + key]
-            words = src[:].rearrange("p u x -> p (u x)").bitcast(F32)
-            for u in range(2):
-                nc.tensor.transpose(et[:, part, u, :], words[:, u * P:(u + 1) * P], ident_f[:])
+        def flip(key, bank, sources):
+            et = psum.tile([P, len(sources), 2, P], F32, tag=bank, name="et")
+            for a, src in enumerate(sources):
+                words = src[:].rearrange("p u x -> p (u x)").bitcast(F32)
+                for u in range(2):
+                    nc.tensor.transpose(et[:, a, u, :], words[:, u * P:(u + 1) * P], ident_f[:])
+            st[("et",) + key] = et
 
-        def evict(key, parts, on_scalar):
-            et = st[("et",) + key]
-            g = gpool.tile([P, parts, P, 4], BF16, tag="g%d" % parts, align_bytes=64)
+        def evict(key, parts):
+            g = gpool.tile([P, parts, P, 4], BF16, tag="g%d" % parts, name="g", align_bytes=64)
             dst = g[:].rearrange("p a n t -> p (a n t)").bitcast(F32).rearrange("p (a n u) -> p a n u", a=parts, u=2)
-            src = et[:].rearrange("p a u n -> p a n u")
-            if on_scalar:
-                nc.scalar.copy(out=dst, in_=src)
-            else:
-                nc.vector.tensor_copy(out=dst, in_=src)
+            nc.scalar.copy(out=dst, in_=st[("et",) + key][:].rearrange("p a u n -> p a n u"))
             st[("g",) + key] = g
 
         def quant(key, parts):
             g = st[("g",) + key]
-            codes = cpool.tile([P, parts * P], U32, tag="codes%d" % parts, align_bytes=64)
-            scl = cpool.tile([P, parts * P], U8, tag="scl%d" % parts, align_bytes=64)
+            codes = cpool.tile([P, parts * P], U32, tag="codes%d" % parts, name="codes", align_bytes=64)
+            scl = cpool.tile([P, parts * P], U8, tag="scl%d" % parts, name="scl", align_bytes=64)
             nc.vector.quantize_mx(out=codes[:].bitcast(FP8X4), scales=scl[:], in_=g[:].rearrange("p a n t -> p (a n t)"))
             st[("c",) + key] = (codes, scl)
 
-        def mx(h, j):
+        def mx(bk):
+            h, j = blocks[bk]
             vset = vsets[h % 2]
-            acc = ps_m.tile([P, TPB, D], F32, tag="misc", name="acc")
+            acc = psum.tile([P, TPB, D], F32, tag="bankA", name="acc")
             for r in range(TPB):
-                codes, scl = st[("c", "w", h, j, r // 2)]
+                codes, scl = st[("c", "w", bk, r // 2)]
                 cols = slice((r % 2) * P, (r % 2 + 1) * P)
                 if r < TPB - 1:
                     rhs, rsc = vset["vwc"][:, r, j, :], vset["vws"][:, r, j, :]
@@ -247,83 +295,119 @@ def tile_slidingwindowattention_kernel(tc, q, k, v, out):
                     rhs=rhs.bitcast(FP8X4), rhs_scale=rsc,
                     start=(r == 0), stop=(j == 0 and r == TPB - 1))
             if j > 0:
-                codes, scl = st[("c", "l", h, j)]
+                codes, scl = st[("c", "l", bk)]
                 nc.tensor.matmul_mx(
                     out=acc[:].rearrange("p r d -> p (r d)"), lhsT=codes[:].bitcast(FP8X4), lhsT_scale=scl[:],
                     rhs=vset["vbc"][:, j - 1, :, :].rearrange("p s d -> p (s d)").bitcast(FP8X4),
                     rhs_scale=vset["vbs"][:, j - 1, :, :].rearrange("p s d -> p (s d)"),
                     start=False, stop=True)
-            st[("acc", h, j)] = acc
+            st[("acc", bk)] = acc
 
-        def fin(h, j):
-            acc = st[("acc", h, j)]
-            den = st[("den", h, j)]
-            rden = small.tile([P, TPB], F32, tag="rden")
+        def den_sum(bk):
+            h, j = blocks[bk]
             if j > 0:
+                den = st[("den", bk)]
                 dsum = small.tile([P, TPB], F32, tag="dsum")
                 nc.gpsimd.tensor_tensor(out=dsum[:], in0=den[:, :, 0], in1=den[:, :, 1], op=ALU.add)
-                nc.vector.reciprocal(out=rden[:], in_=dsum[:])
+                st[("dsum", bk)] = dsum[:]
             else:
-                nc.vector.reciprocal(out=rden[:], in_=den[:, :, 0])
+                st[("dsum", bk)] = st[("den", bk)][:, :, 0]
+
+        def recip(bk):
+            rden = small.tile([P, TPB], F32, tag="rden")
+            nc.vector.reciprocal(out=rden[:], in_=st[("dsum", bk)])
+            st[("rden", bk)] = rden
+
+        def fin(bk):
+            h, j = blocks[bk]
             res = opool.tile([P, TPB, D], F32, tag="res")
-            nc.vector.tensor_tensor(out=res[:], in0=acc[:], in1=rden[:].unsqueeze(2).to_broadcast([P, TPB, D]), op=ALU.mult)
+            nc.vector.tensor_tensor(out=res[:], in0=st[("acc", bk)][:], in1=st[("rden", bk)][:].unsqueeze(2).to_broadcast([P, TPB, D]), op=ALU.mult)
             nc.sync.dma_start(out=out[0, h, j * W:(j + 1) * W, :].rearrange("(r p) d -> p r d", p=P), in_=res[:])
 
-        def ok(x):
-            return 0 <= x < len(tiles)
+        preps = {0: [(0, 1, 4, 4, "bankA")], 2: [(0, 0, 8, 8, "bankC")], 3: [(0, 1, 8, 8, "bankA")]}
+        steps = ((0, 0), (1, 0), (0, 8), (1, 8))
+        for h in range(1, H):
+            s0 = TPH * (h - 1)
+            when = (4, 6, 8, 12) if h == 1 else (0, 4, 8, 12)
+            for s, (which, t0) in zip(when, steps):
+                preps[s0 + s] = preps.get(s0 + s, []) + [(h, which, t0, 8, "bankC")]
 
         def slot(s):
-            x = s - 3
-            if ok(x):
-                h, j, r = tiles[x]
-                if r % 2 == 1:
-                    evict(("w", h, j, r // 2), 2, True)
-                if r == TPB - 1 and j > 0:
-                    evict(("l", h, j), 1, True)
-            x = s - 4
-            if ok(x):
-                h, j, r = tiles[x]
-                if r % 2 == 1:
-                    quant(("w", h, j, r // 2), 2)
-                if r == TPB - 1 and j > 0:
-                    quant(("l", h, j), 1)
-            if ok(s + 1):
-                s_win(s + 1)
-            if ok(s):
-                row_max(s)
-            if ok(s - 1):
-                expo(s - 1)
-            x = s - 2
-            if ok(x):
-                h, j, r = tiles[x]
-                flip(("w", h, j, r // 2), r % 2, 2, ew_tiles[x % N_EW])
-                if r == TPB - 1 and j > 0:
-                    flip(("l", h, j), 0, 1, st[("el", h, j)])
-            x = s - 4
-            if ok(x) and tiles[x][2] == TPB - 1:
-                mx(tiles[x][0], tiles[x][1])
-            x = s - 5
-            if ok(x) and tiles[x][2] == TPB - 1:
-                fin(tiles[x][0], tiles[x][1])
-            if ok(s):
-                h, j, r = tiles[s]
-                if (j, r) == (0, 0) and h + 2 < H:
-                    load(h + 2)
-                if h + 1 < H:
-                    if r == 1:
-                        prep_qk(h + 1, j % 2, j // 2)
-                    if (j, r) == (1, 2):
-                        prep_v(h + 1)
+            r = s % TPB
+            bk = s // TPB
+            h, hs = s // TPH, s % TPH
+            inside = s < len(tiles)
 
-        load(0)
-        load(1)
-        for step in range(2):
-            prep_qk(0, step % 2, step // 2)
-        prep_v(0)
-        for step in range(2, 4):
-            prep_qk(0, step % 2, step // 2)
-        if MANUAL:
-            ctx.enter_context(tc.manual_schedule())
-        s_win(0)
-        for s in range(len(tiles) + 6):
+            def has(b):
+                return 0 <= b < len(blocks)
+
+            if r == 0 and has(bk - 1):
+                evict(("w", bk - 1, 0), 2)
+            if r == 2 and has(bk - 1):
+                evict(("w", bk - 1, 1), 2)
+            if r == 3 and has(bk - 1) and blocks[bk - 1][1] > 0:
+                evict(("l", bk - 1), 1)
+            for args in preps.get(s - 1, []):
+                if args[1] == 1:
+                    prep_copy(*args[:4])
+            if 0 <= s - 1 < len(tiles):
+                expo(s - 1)
+            if s + 1 < len(tiles):
+                scores(s + 1)
+            if r == 3 and has(bk):
+                flip(("w", bk, 0), "bankB", [ew_tiles[(s - 3) % N_EW], ew_tiles[(s - 2) % N_EW]])
+            if r == 1 and has(bk - 1):
+                flip(("w", bk - 1, 1), "bankB", [ew_tiles[(s - 3) % N_EW], ew_tiles[(s - 2) % N_EW]])
+            if r == 1 and has(bk + 1) and blocks[bk + 1][1] > 0:
+                lead_scores(bk + 1)
+            if r == 2 and has(bk - 1) and blocks[bk - 1][1] > 0:
+                flip(("l", bk - 1), "bankC", [st[("el", bk - 1)]])
+            for args in preps.get(s, []):
+                prep_pe(*args)
+            if r == 2 and has(bk - 2):
+                mx(bk - 2)
+            if inside:
+                window_min(s)
+            if r == 2 and has(bk + 1) and blocks[bk + 1][1] > 0:
+                lead_min(bk + 1)
+            if r == 1 and has(bk - 1):
+                quant(("w", bk - 1, 0), 2)
+            if r == 3 and has(bk - 1):
+                quant(("w", bk - 1, 1), 2)
+                recip(bk - 1)
+            if r == 0 and has(bk - 2) and blocks[bk - 2][1] > 0:
+                quant(("l", bk - 2), 1)
+            for args in preps.get(s - 1, []):
+                if args[1] == 0:
+                    prep_copy(*args[:4])
+            if r == 0 and has(bk - 3):
+                fin(bk - 3)
+            if inside:
+                join(s)
+            if r == 1 and has(bk - 1):
+                den_sum(bk - 1)
+            if s in (0, 1):
+                regroup(0, "vector", 2 * s, 2 * s + 2, 0, D)
+            if s == 2:
+                quant_v(0, 0, NB)
+                spread_v(0)
+            if h + 1 < H:
+                if 1 <= hs <= 8:
+                    b, half = (hs - 1) // 2, (hs - 1) % 2
+                    regroup(h + 1, "gpsimd", b, b + 1, half * (D // 2), (half + 1) * (D // 2))
+                if hs == 11:
+                    quant_v(h + 1, 0, 2)
+                if hs == 13:
+                    quant_v(h + 1, 2, 4)
+                    spread_v(h + 1)
+            if hs == 0 and h + 2 < H:
+                load(h + 2)
+
+        prep_pe(0, 0, 0, 8, "bankC")
+        prep_pe(0, 1, 0, 4, "bankA")
+        prep_copy(0, 1, 0, 4)
+        prep_copy(0, 0, 0, 8)
+        make_vset(1)
+        scores(0)
+        for s in range(len(tiles) + 13):
             slot(s)

@@ -34,7 +34,7 @@ def tile_slidingwindowattention_kernel(tc, q, k, v, out):
     with ExitStack() as ctx:
         const = ctx.enter_context(tc.tile_pool(name="const", bufs=1))
         raw = ctx.enter_context(tc.tile_pool(name="raw", bufs=3))
-        tpose = ctx.enter_context(tc.tile_pool(name="tpose", bufs=2))
+        tpose = ctx.enter_context(tc.tile_pool(name="tpose", bufs=3))
         vpool = ctx.enter_context(tc.tile_pool(name="vpool", bufs=2))
         elpool = ctx.enter_context(tc.tile_pool(name="elpool", bufs=3))
         gpool = ctx.enter_context(tc.tile_pool(name="gpool", bufs=4))
@@ -324,13 +324,21 @@ def tile_slidingwindowattention_kernel(tc, q, k, v, out):
             nc.vector.tensor_tensor(out=res[:], in0=st[("acc", bk)][:], in1=st[("rden", bk)][:].unsqueeze(2).to_broadcast([P, TPB, D]), op=ALU.mult)
             nc.sync.dma_start(out=out[0, h, j * W:(j + 1) * W, :].rearrange("(r p) d -> p r d", p=P), in_=res[:])
 
-        preps = {0: [(0, 1, 4, 4, "bankA")], 2: [(0, 0, 8, 8, "bankC")], 3: [(0, 1, 8, 8, "bankA")]}
-        steps = ((0, 0), (1, 0), (0, 8), (1, 8))
-        for h in range(1, H):
+        preps = {
+            -1: [(0, 0, 4, 4, "bankB")],
+            0: [(0, 1, 4, 4, "bankC"), (0, 0, 8, 8, "sl0")],
+            2: [(0, 1, 8, 8, "sl0")],
+            4: [(1, 0, 0, 8, "bankA")],
+            5: [(1, 1, 0, 8, "sl0")],
+            6: [(1, 0, 8, 8, "bankA")],
+            8: [(1, 1, 8, 8, "bankA")],
+        }
+        for h in range(2, H):
             s0 = TPH * (h - 1)
-            when = (4, 6, 8, 12) if h == 1 else (0, 4, 8, 12)
-            for s, (which, t0) in zip(when, steps):
-                preps[s0 + s] = preps.get(s0 + s, []) + [(h, which, t0, 8, "bankC")]
+            preps[s0 - 3] = [(h, 0, 0, 8, "sl0")]
+            preps[s0 - 1] = [(h, 1, 0, 8, "sl0")]
+            preps[s0 + 1] = [(h, 0, 8, 8, "sl0")]
+            preps[s0 + 3] = [(h, 1, 8, 8, "sl0")]
 
         def slot(s):
             r = s % TPB
@@ -338,76 +346,79 @@ def tile_slidingwindowattention_kernel(tc, q, k, v, out):
             h, hs = s // TPH, s % TPH
             inside = s < len(tiles)
 
-            def has(b):
-                return 0 <= b < len(blocks)
+            def has(b, lead=False):
+                return 0 <= b < len(blocks) and (not lead or blocks[b][1] > 0)
 
+            if 0 <= s - 1 < len(tiles):
+                expo(s - 1)
             if r == 0 and has(bk - 1):
                 evict(("w", bk - 1, 0), 2)
             if r == 2 and has(bk - 1):
                 evict(("w", bk - 1, 1), 2)
-            if r == 3 and has(bk - 1) and blocks[bk - 1][1] > 0:
+            if r == 3 and has(bk - 1, True):
                 evict(("l", bk - 1), 1)
             for args in preps.get(s - 1, []):
                 if args[1] == 1:
                     prep_copy(*args[:4])
-            if 0 <= s - 1 < len(tiles):
-                expo(s - 1)
             if s + 1 < len(tiles):
                 scores(s + 1)
             if r == 3 and has(bk):
                 flip(("w", bk, 0), "bankB", [ew_tiles[(s - 3) % N_EW], ew_tiles[(s - 2) % N_EW]])
             if r == 1 and has(bk - 1):
-                flip(("w", bk - 1, 1), "bankB", [ew_tiles[(s - 3) % N_EW], ew_tiles[(s - 2) % N_EW]])
-            if r == 1 and has(bk + 1) and blocks[bk + 1][1] > 0:
+                flip(("w", bk - 1, 1), "bankC", [ew_tiles[(s - 3) % N_EW], ew_tiles[(s - 2) % N_EW]])
+            if r == 2 and has(bk - 1, True):
+                flip(("l", bk - 1), "bankA", [st[("el", bk - 1)]])
+            if r == 2 and has(bk + 1, True):
                 lead_scores(bk + 1)
-            if r == 2 and has(bk - 1) and blocks[bk - 1][1] > 0:
-                flip(("l", bk - 1), "bankC", [st[("el", bk - 1)]])
+            if r == 0 and has(bk - 3):
+                mx(bk - 3)
             for args in preps.get(s, []):
                 prep_pe(*args)
-            if r == 2 and has(bk - 2):
-                mx(bk - 2)
             if inside:
                 window_min(s)
-            if r == 2 and has(bk + 1) and blocks[bk + 1][1] > 0:
+            if r == 3 and has(bk + 1, True):
                 lead_min(bk + 1)
-            if r == 1 and has(bk - 1):
+            if r == 2 and has(bk - 1):
                 quant(("w", bk - 1, 0), 2)
+            if r == 0 and has(bk - 2):
+                quant(("w", bk - 2, 1), 2)
+                if has(bk - 2, True):
+                    quant(("l", bk - 2), 1)
             if r == 3 and has(bk - 1):
-                quant(("w", bk - 1, 1), 2)
                 recip(bk - 1)
-            if r == 0 and has(bk - 2) and blocks[bk - 2][1] > 0:
-                quant(("l", bk - 2), 1)
             for args in preps.get(s - 1, []):
                 if args[1] == 0:
                     prep_copy(*args[:4])
-            if r == 0 and has(bk - 3):
+            if r == 1 and has(bk - 3):
                 fin(bk - 3)
             if inside:
                 join(s)
-            if r == 1 and has(bk - 1):
+            if r == 2 and has(bk - 1):
                 den_sum(bk - 1)
             if s in (0, 1):
                 regroup(0, "vector", 2 * s, 2 * s + 2, 0, D)
             if s == 2:
                 quant_v(0, 0, NB)
                 spread_v(0)
+            if s == 5:
+                make_vset(1)
             if h + 1 < H:
                 if 1 <= hs <= 8:
                     b, half = (hs - 1) // 2, (hs - 1) % 2
                     regroup(h + 1, "gpsimd", b, b + 1, half * (D // 2), (half + 1) * (D // 2))
-                if hs == 11:
-                    quant_v(h + 1, 0, 2)
                 if hs == 13:
+                    quant_v(h + 1, 0, 2)
+                if hs == 15:
                     quant_v(h + 1, 2, 4)
                     spread_v(h + 1)
             if hs == 0 and h + 2 < H:
                 load(h + 2)
 
-        prep_pe(0, 0, 0, 8, "bankC")
+        prep_pe(0, 0, 0, 4, "bankC")
         prep_pe(0, 1, 0, 4, "bankA")
+        prep_copy(0, 0, 0, 4)
         prep_copy(0, 1, 0, 4)
-        prep_copy(0, 0, 0, 8)
-        make_vset(1)
         scores(0)
-        for s in range(len(tiles) + 13):
+        prep_pe(*preps[-1][0])
+        for s in range(len(tiles) + 14):
             slot(s)

@@ -26,7 +26,11 @@ Q = P // TPB
 SCALE = 0.125
 BIG = 2.0 ** 100
 FLOPS = 2 * 2 * H * (2 * NB - 1) * W * W * D
-N_EW = 4
+N_EW = 8
+GROUPS = (((0,), (1,)), ((2,), (3,)))
+GROUPS_FIRST = (((0, 2),), ((1,), (3,)))
+GROUPS_LAST = (((1,), (3,)), ((0, 2),))
+ACC_FIRST = (0, 2, 1, 3)
 
 
 def tile_slidingwindowattention_kernel(tc, q, k, v, out):
@@ -40,12 +44,15 @@ def tile_slidingwindowattention_kernel(tc, q, k, v, out):
         gpool = ctx.enter_context(tc.tile_pool(name="gpool", bufs=4))
         cpool = ctx.enter_context(tc.tile_pool(name="cpool", bufs=6))
         small = ctx.enter_context(tc.tile_pool(name="small", bufs=8))
-        opool = ctx.enter_context(tc.tile_pool(name="opool", bufs=3))
+        opool = ctx.enter_context(tc.tile_pool(name="opool", bufs=6))
         psum = ctx.enter_context(tc.psum_pool(name="psum", bufs=1))
         ctx.enter_context(tc.manual_schedule(engines={ET.PE, ET.Activation, ET.DVE, ET.Pool}))
 
-        def zero(ap):
-            nc.vector.memset(ap.bitcast(I32), 0)
+        def zero(ap, engine="vector"):
+            if engine == "vector":
+                nc.vector.memset(ap.bitcast(I32), 0)
+            else:
+                nc.gpsimd.memset(ap.bitcast(F32), 0.0)
 
         dummy = const.tile([P, 2], F32)
         nc.vector.memset(dummy[:], 0.0)
@@ -110,7 +117,7 @@ def tile_slidingwindowattention_kernel(tc, q, k, v, out):
 
         vsets = []
 
-        def make_vset(i):
+        def make_vset(i, engine):
             vset = {
                 "vq": const.tile([P, NB, D], U32, name="vq%d" % i, align_bytes=64),
                 "vs": const.tile([P, NB, D], U8, name="vs%d" % i, align_bytes=64),
@@ -118,15 +125,20 @@ def tile_slidingwindowattention_kernel(tc, q, k, v, out):
                 "vws": const.tile([P, TPB - 1, NB, D], U8, name="vws%d" % i, align_bytes=64),
                 "vbc": const.tile([P, NB - 1, TPB, D], U32, name="vbc%d" % i, align_bytes=64),
                 "vbs": const.tile([P, NB - 1, TPB, D], U8, name="vbs%d" % i, align_bytes=64),
+                "vpc": const.tile([P, 2, D], U32, name="vpc%d" % i, align_bytes=64),
+                "vps": const.tile([P, 2, D], U8, name="vps%d" % i, align_bytes=64),
             }
-            zero(vset["vs"][:].rearrange("p b d -> p (b d)"))
-            zero(vset["vwc"][:, :, 0, :])
-            zero(vset["vws"][:, :, 0, :])
-            zero(vset["vbc"][:].rearrange("p a b d -> p (a b d)"))
-            zero(vset["vbs"][:].rearrange("p a b d -> p (a b d)"))
+            zero(vset["vs"][:].rearrange("p b d -> p (b d)"), engine)
+            zero(vset["vwc"][:, 1, 0, :], engine)
+            zero(vset["vws"][:, 1, 0, :], engine)
+            zero(vset["vpc"][:].rearrange("p a d -> p (a d)"), engine)
+            zero(vset["vps"][:].rearrange("p a d -> p (a d)"), engine)
+            zero(vset["vbc"][:].rearrange("p a b d -> p (a b d)"), engine)
+            zero(vset["vbs"][:].rearrange("p a b d -> p (a b d)"), engine)
             vsets.append(vset)
 
-        make_vset(0)
+        make_vset(0, "vector")
+        make_vset(1, "gpsimd")
         mask = const.tile([P, 2, 2, 2 * Q], BF16)
         nc.vector.tensor_copy(out=mask[:].rearrange("p m u x -> p m (u x)"), in_=mask_f[:])
         ew_tiles = []
@@ -179,19 +191,28 @@ def tile_slidingwindowattention_kernel(tc, q, k, v, out):
 
         def spread_v(h):
             vset = vsets[h % 2]
-            for src_n, win_n, bd_n in (("vq", "vwc", "vbc"), ("vs", "vws", "vbs")):
+            for src_n, win_n, bd_n, pk_n in (("vq", "vwc", "vbc", "vpc"), ("vs", "vws", "vbs", "vps")):
                 src = vset[src_n][:].bitcast(I32)
                 win = vset[win_n][:].bitcast(I32)
                 bd = vset[bd_n][:].bitcast(I32)
+                pk = vset[pk_n][:].bitcast(I32)
+                nc.sync.dma_start(out=pk[3 * Q:P, 0, :], in_=src[0:Q, 0, :])
+                nc.sync.dma_start(out=pk[0:3 * Q, 1, :], in_=src[0:3 * Q, 0, :])
                 for r in range(TPB - 1):
                     cut = Q * (r + 1)
-                    nc.sync.dma_start(out=win[0:cut, r, :, :], in_=src[0:cut, :, :])
+                    b0 = 0 if r == 1 else 1
+                    nc.sync.dma_start(out=win[0:cut, r, b0:NB, :], in_=src[0:cut, b0:NB, :])
                     nc.sync.dma_start(out=win[cut:P, r, 1:NB, :], in_=src[cut:P, 0:NB - 1, :])
                 for s in range(TPB):
                     nc.sync.dma_start(out=bd[Q * s:Q * (s + 1), :, s, :], in_=src[Q * s:Q * (s + 1), 0:NB - 1, :])
 
-        tiles = [(h, j, r) for h in range(H) for j in range(NB) for r in range(TPB)]
-        blocks = [(h, j) for h in range(H) for j in range(NB)]
+        blocks = [(h, j) for h in range(H - 1) for j in range(NB)] + [(H - 1, j) for j in (1, 2, 3, 0)]
+        last = len(blocks) - 1
+
+        def groups(bk):
+            return GROUPS if blocks[bk][1] > 0 else GROUPS_LAST if bk == last else GROUPS_FIRST
+
+        tiles = [(h, j, r) for bk, (h, j) in enumerate(blocks) for g in groups(bk) for w in g for r in w]
 
         def kT_view(h):
             return heads[h]["kT"][:].rearrange("d (b u x) -> d b u x", u=2, x=2 * P)
@@ -243,16 +264,25 @@ def tile_slidingwindowattention_kernel(tc, q, k, v, out):
                 nc.gpsimd.tensor_scalar(out=nb[:], in0=st[("nb", x)][:], scalar1=st[("nbl", x // TPB)][:, r:r + 1], scalar2=None, op0=ALU.min)
                 st[("nb", x)] = nb
 
+        def ew_tile(bk, r):
+            return ew_tiles[(TPB * bk + r) % N_EW]
+
+        def place(bk, r):
+            return r if blocks[bk][1] > 0 else ACC_FIRST.index(r)
+
         def expo(x):
             h, j, r = tiles[x]
             bk = x // TPB
             nb = st[("nb", x)]
-            if r == 0:
+            if x % TPB == 0:
                 st[("den", bk)] = small.tile([P, TPB, 2], F32, tag="den", name="den")
                 if j > 0:
                     st[("el", bk)] = elpool.tile([P, 2, 2 * P], BF16, tag="el", name="el")
             den = st[("den", bk)]
-            nc.scalar.activation(out=ew_tiles[x % N_EW][:, :, 0:seen(x)], in_=st[("sw", x)][:, :, 0:seen(x)], func=ACTF.Exp, bias=nb[:], scale=-1.0, accum_out=den[:, r, 0:1])
+            r_to, c_to = (2, 3 * 2 * Q) if (j, r) == (0, 0) else (r, 0)
+            nc.scalar.activation(
+                out=ew_tile(bk, r_to)[:, :, c_to:c_to + seen(x)], in_=st[("sw", x)][:, :, 0:seen(x)],
+                func=ACTF.Exp, bias=nb[:], scale=-1.0, accum_out=den[:, place(bk, r), 0:1])
             if j > 0:
                 nc.scalar.activation(
                     out=st[("el", bk)][:, :, 2 * Q * r:2 * Q * (r + 1)], in_=st[("sl", bk)][:, r, :, :],
@@ -265,6 +295,15 @@ def tile_slidingwindowattention_kernel(tc, q, k, v, out):
                 for u in range(2):
                     nc.tensor.transpose(et[:, a, u, :], words[:, u * P:(u + 1) * P], ident_f[:])
             st[("et",) + key] = et
+
+        def flip_group(bk, gi, bank):
+            flip(("w", bk, gi), bank, [ew_tile(bk, w[-1]) for w in groups(bk)[gi]])
+
+        def evict_group(bk, gi):
+            evict(("w", bk, gi), len(groups(bk)[gi]))
+
+        def quant_group(bk, gi):
+            quant(("w", bk, gi), len(groups(bk)[gi]))
 
         def evict(key, parts):
             g = gpool.tile([P, parts, P, 4], BF16, tag="g%d" % parts, name="g", align_bytes=64)
@@ -279,21 +318,27 @@ def tile_slidingwindowattention_kernel(tc, q, k, v, out):
             nc.vector.quantize_mx(out=codes[:].bitcast(FP8X4), scales=scl[:], in_=g[:].rearrange("p a n t -> p (a n t)"))
             st[("c",) + key] = (codes, scl)
 
-        def mx(bk):
+        def mx(bk, gis=(0, 1), bank="bankA"):
             h, j = blocks[bk]
             vset = vsets[h % 2]
-            acc = psum.tile([P, TPB, D], F32, tag="bankA", name="acc")
-            for r in range(TPB):
-                codes, scl = st[("c", "w", bk, r // 2)]
-                cols = slice((r % 2) * P, (r % 2 + 1) * P)
-                if r < TPB - 1:
-                    rhs, rsc = vset["vwc"][:, r, j, :], vset["vws"][:, r, j, :]
-                else:
-                    rhs, rsc = vset["vq"][:, j, :], vset["vs"][:, j, :]
-                nc.tensor.matmul_mx(
-                    out=acc[:, r, :], lhsT=codes[:, cols].bitcast(FP8X4), lhsT_scale=scl[:, cols],
-                    rhs=rhs.bitcast(FP8X4), rhs_scale=rsc,
-                    start=(r == 0), stop=(j == 0 and r == TPB - 1))
+            acc = psum.tile([P, TPB, D], F32, tag=bank, name="acc")
+            for gi in gis:
+                codes, scl = st[("c", "w", bk, gi)]
+                for a, w in enumerate(groups(bk)[gi]):
+                    r = w[-1]
+                    cols = slice(a * P, (a + 1) * P)
+                    if len(w) == 2:
+                        rhs, rsc = vset["vpc"][:].rearrange("p a d -> p (a d)"), vset["vps"][:].rearrange("p a d -> p (a d)")
+                    elif r < TPB - 1:
+                        rhs, rsc = vset["vwc"][:, r, j, :], vset["vws"][:, r, j, :]
+                    else:
+                        rhs, rsc = vset["vq"][:, j, :], vset["vs"][:, j, :]
+                    p0 = place(bk, w[0])
+                    nc.tensor.matmul_mx(
+                        out=acc[:, p0:p0 + len(w), :].rearrange("p r d -> p (r d)"),
+                        lhsT=codes[:, cols].bitcast(FP8X4), lhsT_scale=scl[:, cols],
+                        rhs=rhs.bitcast(FP8X4), rhs_scale=rsc,
+                        start=(j == 0 or r == 0), stop=(j == 0))
             if j > 0:
                 codes, scl = st[("c", "l", bk)]
                 nc.tensor.matmul_mx(
@@ -301,7 +346,7 @@ def tile_slidingwindowattention_kernel(tc, q, k, v, out):
                     rhs=vset["vbc"][:, j - 1, :, :].rearrange("p s d -> p (s d)").bitcast(FP8X4),
                     rhs_scale=vset["vbs"][:, j - 1, :, :].rearrange("p s d -> p (s d)"),
                     start=False, stop=True)
-            st[("acc", bk)] = acc
+            st[("acc", bk, gis[-1])] = acc
 
         def den_sum(bk):
             h, j = blocks[bk]
@@ -318,11 +363,20 @@ def tile_slidingwindowattention_kernel(tc, q, k, v, out):
             nc.vector.reciprocal(out=rden[:], in_=st[("dsum", bk)])
             st[("rden", bk)] = rden
 
-        def fin(bk):
+        def fin(bk, gis=(0, 1)):
             h, j = blocks[bk]
+            used = [place(bk, r) for gi in gis for w in groups(bk)[gi] for r in w]
+            p0, p1 = min(used), max(used) + 1
             res = opool.tile([P, TPB, D], F32, tag="res")
-            nc.vector.tensor_tensor(out=res[:], in0=st[("acc", bk)][:], in1=st[("rden", bk)][:].unsqueeze(2).to_broadcast([P, TPB, D]), op=ALU.mult)
-            nc.sync.dma_start(out=out[0, h, j * W:(j + 1) * W, :].rearrange("(r p) d -> p r d", p=P), in_=res[:])
+            nc.vector.tensor_tensor(
+                out=res[:, p0:p1, :], in0=st[("acc", bk, gis[-1])][:, p0:p1, :],
+                in1=st[("rden", bk)][:, p0:p1].unsqueeze(2).to_broadcast([P, p1 - p0, D]), op=ALU.mult)
+            rows = out[0, h, j * W:(j + 1) * W, :]
+            if j > 0:
+                nc.sync.dma_start(out=rows.rearrange("(r p) d -> p r d", p=P), in_=res[:])
+            else:
+                for a in range(p0 // 2, p1 // 2):
+                    nc.sync.dma_start(out=rows.rearrange("(b a p) d -> a p b d", a=2, p=P)[a], in_=res[:, 2 * a:2 * a + 2, :])
 
         preps = {
             -1: [(0, 0, 4, 4, "bankB")],
@@ -352,9 +406,9 @@ def tile_slidingwindowattention_kernel(tc, q, k, v, out):
             if 0 <= s - 1 < len(tiles):
                 expo(s - 1)
             if r == 0 and has(bk - 1):
-                evict(("w", bk - 1, 0), 2)
+                evict_group(bk - 1, 0)
             if r == 2 and has(bk - 1):
-                evict(("w", bk - 1, 1), 2)
+                evict_group(bk - 1, 1)
             if r == 3 and has(bk - 1, True):
                 evict(("l", bk - 1), 1)
             for args in preps.get(s - 1, []):
@@ -363,15 +417,21 @@ def tile_slidingwindowattention_kernel(tc, q, k, v, out):
             if s + 1 < len(tiles):
                 scores(s + 1)
             if r == 3 and has(bk):
-                flip(("w", bk, 0), "bankB", [ew_tiles[(s - 3) % N_EW], ew_tiles[(s - 2) % N_EW]])
+                flip_group(bk, 0, "bankB")
             if r == 1 and has(bk - 1):
-                flip(("w", bk - 1, 1), "bankC", [ew_tiles[(s - 3) % N_EW], ew_tiles[(s - 2) % N_EW]])
+                flip_group(bk - 1, 1, "bankC")
             if r == 2 and has(bk - 1, True):
                 flip(("l", bk - 1), "bankA", [st[("el", bk - 1)]])
             if r == 2 and has(bk + 1, True):
                 lead_scores(bk + 1)
-            if r == 0 and has(bk - 3):
+            if r == 0 and has(bk - 3) and bk - 3 < last - 1:
                 mx(bk - 3)
+            if s == TPB * last + 5:
+                mx(last - 1)
+            if s == TPB * last + 7:
+                mx(last, (0,), "bankB")
+            if s == TPB * last + 8:
+                mx(last, (1,))
             for args in preps.get(s, []):
                 prep_pe(*args)
             if inside:
@@ -379,29 +439,37 @@ def tile_slidingwindowattention_kernel(tc, q, k, v, out):
             if r == 3 and has(bk + 1, True):
                 lead_min(bk + 1)
             if r == 2 and has(bk - 1):
-                quant(("w", bk - 1, 0), 2)
-            if r == 0 and has(bk - 2):
-                quant(("w", bk - 2, 1), 2)
+                quant_group(bk - 1, 0)
+            if r == 0 and has(bk - 2) and bk - 2 < last:
+                quant_group(bk - 2, 1)
                 if has(bk - 2, True):
                     quant(("l", bk - 2), 1)
+            if s == TPB * last + 7:
+                quant_group(last, 1)
             if r == 3 and has(bk - 1):
                 recip(bk - 1)
             for args in preps.get(s - 1, []):
                 if args[1] == 0:
                     prep_copy(*args[:4])
-            if r == 1 and has(bk - 3):
+            if r == 1 and has(bk - 3) and bk - 3 < last - 1:
                 fin(bk - 3)
+            if s == TPB * last + 6:
+                fin(last - 1)
+            if s == TPB * last + 8:
+                fin(last, (0,))
+            if s == TPB * last + 9:
+                fin(last, (1,))
             if inside:
                 join(s)
             if r == 2 and has(bk - 1):
                 den_sum(bk - 1)
+            if s == 0:
+                regroup(0, "vector", 0, 2, 0, D)
             if s in (0, 1):
-                regroup(0, "vector", 2 * s, 2 * s + 2, 0, D)
+                regroup(0, "gpsimd", 2 + s, 3 + s, 0, D)
             if s == 2:
                 quant_v(0, 0, NB)
                 spread_v(0)
-            if s == 5:
-                make_vset(1)
             if h + 1 < H:
                 if 1 <= hs <= 8:
                     b, half = (hs - 1) // 2, (hs - 1) % 2
@@ -420,5 +488,5 @@ def tile_slidingwindowattention_kernel(tc, q, k, v, out):
         prep_copy(0, 1, 0, 4)
         scores(0)
         prep_pe(*preps[-1][0])
-        for s in range(len(tiles) + 14):
+        for s in range(len(tiles) + 6):
             slot(s)

@@ -48,11 +48,8 @@ def tile_slidingwindowattention_kernel(tc, q, k, v, out):
         psum = ctx.enter_context(tc.psum_pool(name="psum", bufs=1))
         ctx.enter_context(tc.manual_schedule(engines={ET.PE, ET.Activation, ET.DVE, ET.Pool}))
 
-        def zero(ap, engine="vector"):
-            if engine == "vector":
-                nc.vector.memset(ap.bitcast(I32), 0)
-            else:
-                nc.gpsimd.memset(ap.bitcast(F32), 0.0)
+        def zero(ap):
+            nc.vector.memset(ap.bitcast(I32), 0)
 
         dummy = const.tile([P, 2], F32)
         nc.vector.memset(dummy[:], 0.0)
@@ -60,16 +57,17 @@ def tile_slidingwindowattention_kernel(tc, q, k, v, out):
 
         ident = const.tile([P, P], BF16)
         make_identity(nc, ident[:])
-        mask_f = const.tile([P, 2, P], F32)
-        nc.gpsimd.memset(mask_f[:], 0.0)
+        mask = const.tile([P, 2, P], BF16)
+        nc.vector.memset(mask[:], 0.0)
         nc.gpsimd.affine_select(
-            out=mask_f[:, 0, :], in_=mask_f[:, 0, :], compare_op=ALU.is_ge, fill=BIG,
+            out=mask[:, 0, :], in_=mask[:, 0, :], compare_op=ALU.is_ge, fill=BIG,
             base=0, pattern=[[-1, 2], [-4, Q], [-2, 2]], channel_multiplier=1,
         )
         nc.gpsimd.affine_select(
-            out=mask_f[:, 1, :], in_=mask_f[:, 1, :], compare_op=ALU.is_ge, fill=BIG,
+            out=mask[:, 1, :], in_=mask[:, 1, :], compare_op=ALU.is_ge, fill=BIG,
             base=-1, pattern=[[1, 2], [4, Q], [2, 2]], channel_multiplier=-1,
         )
+        mask_v = mask[:].rearrange("p m (u x) -> p m u x", u=2)
         ident_f = const.tile([P, P], F32)
         make_identity(nc, ident_f[:])
 
@@ -117,7 +115,7 @@ def tile_slidingwindowattention_kernel(tc, q, k, v, out):
 
         vsets = []
 
-        def make_vset(i, engine):
+        def make_vset(i):
             vset = {
                 "vq": const.tile([P, NB, D], U32, name="vq%d" % i, align_bytes=64),
                 "vs": const.tile([P, NB, D], U8, name="vs%d" % i, align_bytes=64),
@@ -128,24 +126,22 @@ def tile_slidingwindowattention_kernel(tc, q, k, v, out):
                 "vpc": const.tile([P, 2, D], U32, name="vpc%d" % i, align_bytes=64),
                 "vps": const.tile([P, 2, D], U8, name="vps%d" % i, align_bytes=64),
             }
-            zero(vset["vs"][:].rearrange("p b d -> p (b d)"), engine)
-            zero(vset["vwc"][:, 1, 0, :], engine)
-            zero(vset["vws"][:, 1, 0, :], engine)
-            zero(vset["vpc"][:].rearrange("p a d -> p (a d)"), engine)
-            zero(vset["vps"][:].rearrange("p a d -> p (a d)"), engine)
-            zero(vset["vbc"][:].rearrange("p a b d -> p (a b d)"), engine)
-            zero(vset["vbs"][:].rearrange("p a b d -> p (a b d)"), engine)
+            zero(vset["vs"][:].rearrange("p b d -> p (b d)"))
+            zero(vset["vwc"][:, 1, 0, :])
+            zero(vset["vws"][:, 1, 0, :])
+            zero(vset["vpc"][:].rearrange("p a d -> p (a d)"))
+            zero(vset["vps"][:].rearrange("p a d -> p (a d)"))
+            zero(vset["vbc"][:].rearrange("p a b d -> p (a b d)"))
+            zero(vset["vbs"][:].rearrange("p a b d -> p (a b d)"))
             vsets.append(vset)
 
-        make_vset(0, "vector")
-        make_vset(1, "gpsimd")
-        mask = const.tile([P, 2, 2, 2 * Q], BF16)
-        nc.vector.tensor_copy(out=mask[:].rearrange("p m u x -> p m (u x)"), in_=mask_f[:])
+        make_vset(0)
         ew_tiles = []
         for i in range(N_EW):
             ew0 = const.tile([P, 2, 2 * P], BF16, name="ew%d" % i)
-            zero(ew0[:].rearrange("p u x -> p (u x)"))
             ew_tiles.append(ew0)
+        zero(ew_tiles[1][:].rearrange("p u x -> p (u x)"))
+        make_vset(1)
 
         def prep_pe(h, which, t0, n, bank):
             src = heads[h]["qr" if which == 0 else "kr"]
@@ -224,7 +220,7 @@ def tile_slidingwindowattention_kernel(tc, q, k, v, out):
             for r in range(TPB):
                 i = TPB * j + r
                 nc.tensor.matmul(sl[:, r, :, :], lhsT=hd["qT"][:, i * P:(i + 1) * P], rhs=kT_view(h)[:, j - 1, :, 2 * Q * r:2 * Q * (r + 1)], start=True, stop=False)
-                nc.tensor.matmul(sl[:, r, :, :], lhsT=ident[:], rhs=mask[:, 1, :, :], start=False, stop=True)
+                nc.tensor.matmul(sl[:, r, :, :], lhsT=ident[:], rhs=mask_v[:, 1, :, :], start=False, stop=True)
             st[("sl", bk)] = sl
 
         def lead_min(bk):
@@ -237,11 +233,11 @@ def tile_slidingwindowattention_kernel(tc, q, k, v, out):
             i = TPB * j + r
             qcols = heads[h]["qT"][:, i * P:(i + 1) * P]
             cut = 2 * Q * (r + 1)
-            sw = psum.tile([P, 2, 2 * P], F32, tag="sw%d" % (x % 3), name="sw")
+            sw = psum.tile([P, 2, 2 * P], F32, tag="sw%d" % (x % 4), name="sw")
             nc.tensor.matmul(sw[:, :, 0:cut], lhsT=qcols, rhs=kT_view(h)[:, j, :, 0:cut], start=True, stop=False)
             if j > 0 and cut < 2 * P:
                 nc.tensor.matmul(sw[:, :, cut:2 * P], lhsT=qcols, rhs=kT_view(h)[:, j - 1, :, cut:2 * P], start=False, stop=False)
-            nc.tensor.matmul(sw[:, :, cut - 2 * Q:cut], lhsT=ident[:], rhs=mask[:, 0, :, :], start=False, stop=True)
+            nc.tensor.matmul(sw[:, :, cut - 2 * Q:cut], lhsT=ident[:], rhs=mask_v[:, 0, :, :], start=False, stop=True)
             st[("sw", x)] = sw
 
         def seen(x):
@@ -300,15 +296,15 @@ def tile_slidingwindowattention_kernel(tc, q, k, v, out):
             flip(("w", bk, gi), bank, [ew_tile(bk, w[-1]) for w in groups(bk)[gi]])
 
         def evict_group(bk, gi):
-            evict(("w", bk, gi), len(groups(bk)[gi]))
+            evict(("w", bk, gi), len(groups(bk)[gi]), nc.scalar.copy)
 
         def quant_group(bk, gi):
             quant(("w", bk, gi), len(groups(bk)[gi]))
 
-        def evict(key, parts):
+        def evict(key, parts, copy):
             g = gpool.tile([P, parts, P, 4], BF16, tag="g%d" % parts, name="g", align_bytes=64)
             dst = g[:].rearrange("p a n t -> p (a n t)").bitcast(F32).rearrange("p (a n u) -> p a n u", a=parts, u=2)
-            nc.scalar.copy(out=dst, in_=st[("et",) + key][:].rearrange("p a u n -> p a n u"))
+            copy(out=dst, in_=st[("et",) + key][:].rearrange("p a u n -> p a n u"))
             st[("g",) + key] = g
 
         def quant(key, parts):
@@ -380,7 +376,7 @@ def tile_slidingwindowattention_kernel(tc, q, k, v, out):
 
         preps = {
             -1: [(0, 0, 4, 4, "bankB")],
-            0: [(0, 1, 4, 4, "bankC"), (0, 0, 8, 8, "sl0")],
+            0: [(0, 1, 4, 4, "sl1"), (0, 0, 8, 8, "sl0")],
             2: [(0, 1, 8, 8, "sl0")],
             4: [(1, 0, 0, 8, "bankA")],
             5: [(1, 1, 0, 8, "sl0")],
@@ -393,6 +389,9 @@ def tile_slidingwindowattention_kernel(tc, q, k, v, out):
             preps[s0 - 1] = [(h, 1, 0, 8, "sl0")]
             preps[s0 + 1] = [(h, 0, 8, 8, "sl0")]
             preps[s0 + 3] = [(h, 1, 8, 8, "sl0")]
+
+        def lead_on_vector(bk):
+            return blocks[bk][1] >= 2
 
         def slot(s):
             r = s % TPB
@@ -409,17 +408,17 @@ def tile_slidingwindowattention_kernel(tc, q, k, v, out):
                 evict_group(bk - 1, 0)
             if r == 2 and has(bk - 1):
                 evict_group(bk - 1, 1)
-            if r == 3 and has(bk - 1, True):
-                evict(("l", bk - 1), 1)
+            if r == 3 and has(bk - 1, True) and not lead_on_vector(bk - 1):
+                evict(("l", bk - 1), 1, nc.scalar.copy)
             for args in preps.get(s - 1, []):
                 if args[1] == 1:
                     prep_copy(*args[:4])
-            if s + 1 < len(tiles):
-                scores(s + 1)
+            if s + 2 < len(tiles):
+                scores(s + 2)
             if r == 3 and has(bk):
                 flip_group(bk, 0, "bankB")
             if r == 1 and has(bk - 1):
-                flip_group(bk - 1, 1, "bankC")
+                flip_group(bk - 1, 1, "bankB")
             if r == 2 and has(bk - 1, True):
                 flip(("l", bk - 1), "bankA", [st[("el", bk - 1)]])
             if r == 2 and has(bk + 1, True):
@@ -434,8 +433,8 @@ def tile_slidingwindowattention_kernel(tc, q, k, v, out):
                 mx(last, (1,))
             for args in preps.get(s, []):
                 prep_pe(*args)
-            if inside:
-                window_min(s)
+            if s + 1 < len(tiles):
+                window_min(s + 1)
             if r == 3 and has(bk + 1, True):
                 lead_min(bk + 1)
             if r == 2 and has(bk - 1):
@@ -459,21 +458,23 @@ def tile_slidingwindowattention_kernel(tc, q, k, v, out):
                 fin(last, (0,))
             if s == TPB * last + 9:
                 fin(last, (1,))
-            if inside:
-                join(s)
+            if r == 3 and has(bk - 1, True) and lead_on_vector(bk - 1):
+                evict(("l", bk - 1), 1, nc.vector.tensor_copy)
+            if s + 1 < len(tiles):
+                join(s + 1)
             if r == 2 and has(bk - 1):
                 den_sum(bk - 1)
-            if s == 0:
-                regroup(0, "vector", 0, 2, 0, D)
             if s in (0, 1):
-                regroup(0, "gpsimd", 2 + s, 3 + s, 0, D)
+                regroup(0, "vector", 2 * s, 2 * s + 2, 0, D)
             if s == 2:
                 quant_v(0, 0, NB)
                 spread_v(0)
             if h + 1 < H:
-                if 1 <= hs <= 8:
-                    b, half = (hs - 1) // 2, (hs - 1) % 2
-                    regroup(h + 1, "gpsimd", b, b + 1, half * (D // 2), (half + 1) * (D // 2))
+                if h == 0 and 5 <= hs <= 12:
+                    b, half = (hs - 5) // 2, (hs - 5) % 2
+                    regroup(1, "gpsimd", b, b + 1, half * (D // 2), (half + 1) * (D // 2))
+                if h > 0 and hs < NB:
+                    regroup(h + 1, "gpsimd", hs, hs + 1, 0, D)
                 if hs == 13:
                     quant_v(h + 1, 0, 2)
                 if hs == 15:
@@ -482,11 +483,13 @@ def tile_slidingwindowattention_kernel(tc, q, k, v, out):
             if hs == 0 and h + 2 < H:
                 load(h + 2)
 
-        prep_pe(0, 0, 0, 4, "bankC")
+        prep_pe(0, 0, 0, 4, "sl0")
         prep_pe(0, 1, 0, 4, "bankA")
         prep_copy(0, 0, 0, 4)
         prep_copy(0, 1, 0, 4)
         scores(0)
+        scores(1)
+        window_min(0)
         prep_pe(*preps[-1][0])
         for s in range(len(tiles) + 6):
             slot(s)

@@ -60,11 +60,11 @@ def tile_slidingwindowattention_kernel(tc, q, k, v, out):
         mask = const.tile([P, 2, P], BF16)
         nc.vector.memset(mask[:], 0.0)
         nc.gpsimd.affine_select(
-            out=mask[:, 0, :], in_=mask[:, 0, :], compare_op=ALU.is_ge, fill=BIG,
+            out=mask[:, 0, :], in_=mask[:, 0, :], compare_op=ALU.is_ge, fill=-BIG,
             base=0, pattern=[[-1, 2], [-4, Q], [-2, 2]], channel_multiplier=1,
         )
         nc.gpsimd.affine_select(
-            out=mask[:, 1, :], in_=mask[:, 1, :], compare_op=ALU.is_ge, fill=BIG,
+            out=mask[:, 1, :], in_=mask[:, 1, :], compare_op=ALU.is_ge, fill=-BIG,
             base=-1, pattern=[[1, 2], [4, Q], [2, 2]], channel_multiplier=-1,
         )
         mask_v = mask[:].rearrange("p m (u x) -> p m u x", u=2)
@@ -154,25 +154,26 @@ def tile_slidingwindowattention_kernel(tc, q, k, v, out):
                 nc.tensor.transpose(pt[:, i * P:(i + 1) * P], src[:, t, :], ident[:])
             st[("pt", h, which, t0)] = pt
 
+        def prep_on_vector(h, which, t0):
+            return which == 0 and (h % 2 or t0 < 8)
+
         def prep_copy(h, which, t0, n):
             nm = "qT" if which == 0 else "kT"
             if t0 == 0:
                 heads[h][nm] = tpose.tile([P, N], BF16, tag=nm, name=nm)
             dst = heads[h][nm][:, P * t0:P * (t0 + n)]
             pt = st[("pt", h, which, t0)]
-            if which == 0:
-                nc.vector.tensor_scalar(out=dst, in0=pt[:, 0:n * P], scalar1=-SCALE, scalar2=None, op0=ALU.mult)
-            else:
-                nc.scalar.copy(out=dst, in_=pt[:, 0:n * P])
+            copy = nc.vector.tensor_copy if prep_on_vector(h, which, t0) else nc.scalar.copy
+            copy(out=dst, in_=pt[:, 0:n * P])
 
-        def regroup(h, engine, b0, b1, d0, d1):
+        def regroup(h, b0, b1, d0, d1, on_scalar=False):
             if "vg" not in heads[h]:
                 heads[h]["vg"] = vpool.tile([P, NB, D, 4], BF16, tag="vg", name="vg", align_bytes=64)
             dst = heads[h]["vg"][:].rearrange("p b d (u e) -> p b d u e", e=2)
             src = heads[h]["vr"][:].rearrange("p (b e u) d -> p b d u e", e=2, u=2)
             for b in range(b0, b1):
-                if engine == "vector":
-                    nc.vector.tensor_copy(out=dst[:, b, d0:d1], in_=src[:, b, d0:d1])
+                if on_scalar:
+                    nc.scalar.copy(out=dst[:, b, d0:d1], in_=src[:, b, d0:d1])
                 else:
                     nc.gpsimd.tensor_scalar(out=dst[:, b, d0:d1], in0=src[:, b, d0:d1], scalar1=1.0, scalar2=0.0, op0=ALU.mult, op1=ALU.add)
 
@@ -223,10 +224,10 @@ def tile_slidingwindowattention_kernel(tc, q, k, v, out):
                 nc.tensor.matmul(sl[:, r, :, :], lhsT=ident[:], rhs=mask_v[:, 1, :, :], start=False, stop=True)
             st[("sl", bk)] = sl
 
-        def lead_min(bk):
-            nbl = small.tile([P, TPB], F32, tag="nbl")
-            nc.vector.tensor_reduce(out=nbl[:], in_=st[("sl", bk)][:].rearrange("p r u x -> p r (u x)"), axis=AX.X, op=ALU.min)
-            st[("nbl", bk)] = nbl
+        def lead_max(bk):
+            mxl = small.tile([P, TPB], F32, tag="mxl")
+            nc.vector.tensor_reduce(out=mxl[:], in_=st[("sl", bk)][:].rearrange("p r u x -> p r (u x)"), axis=AX.X, op=ALU.max)
+            st[("mxl", bk)] = mxl
 
         def scores(x):
             h, j, r = tiles[x]
@@ -244,21 +245,23 @@ def tile_slidingwindowattention_kernel(tc, q, k, v, out):
             h, j, r = tiles[x]
             return 2 * P if j > 0 else 2 * Q * (r + 1)
 
-        def window_min(x):
-            nbw = small.tile([P, 1], F32, tag="nbw")
+        def window_max(x):
+            mxw = small.tile([P, 1], F32, tag="mxw")
             sw = st[("sw", x)]
             if seen(x) == 2 * P:
-                nc.vector.tensor_reduce(out=nbw[:], in_=sw[:].rearrange("p u x -> p (u x)"), axis=AX.X, op=ALU.min)
+                nc.vector.tensor_reduce(out=mxw[:], in_=sw[:].rearrange("p u x -> p (u x)"), axis=AX.X, op=ALU.max)
             else:
-                nc.vector.tensor_reduce(out=nbw[:], in_=sw[:, :, 0:seen(x)], axis=AX.XY, op=ALU.min)
-            st[("nb", x)] = nbw
+                nc.vector.tensor_reduce(out=mxw[:], in_=sw[:, :, 0:seen(x)], axis=AX.XY, op=ALU.max)
+            st[("mx", x)] = mxw
 
         def join(x):
             h, j, r = tiles[x]
+            nb = small.tile([P, 1], F32, tag="nb")
             if j > 0:
-                nb = small.tile([P, 1], F32, tag="nb")
-                nc.gpsimd.tensor_scalar(out=nb[:], in0=st[("nb", x)][:], scalar1=st[("nbl", x // TPB)][:, r:r + 1], scalar2=None, op0=ALU.min)
-                st[("nb", x)] = nb
+                nc.gpsimd.tensor_scalar(out=nb[:], in0=st[("mx", x)][:], scalar1=st[("mxl", x // TPB)][:, r:r + 1], scalar2=-SCALE, op0=ALU.max, op1=ALU.mult)
+            else:
+                nc.gpsimd.tensor_scalar(out=nb[:], in0=st[("mx", x)][:], scalar1=-SCALE, scalar2=0.0, op0=ALU.mult, op1=ALU.add)
+            st[("nb", x)] = nb
 
         def ew_tile(bk, r):
             return ew_tiles[(TPB * bk + r) % N_EW]
@@ -278,11 +281,11 @@ def tile_slidingwindowattention_kernel(tc, q, k, v, out):
             r_to, c_to = (2, 3 * 2 * Q) if (j, r) == (0, 0) else (r, 0)
             nc.scalar.activation(
                 out=ew_tile(bk, r_to)[:, :, c_to:c_to + seen(x)], in_=st[("sw", x)][:, :, 0:seen(x)],
-                func=ACTF.Exp, bias=nb[:], scale=-1.0, accum_out=den[:, place(bk, r), 0:1])
+                func=ACTF.Exp, bias=nb[:], scale=SCALE, accum_out=den[:, place(bk, r), 0:1])
             if j > 0:
                 nc.scalar.activation(
                     out=st[("el", bk)][:, :, 2 * Q * r:2 * Q * (r + 1)], in_=st[("sl", bk)][:, r, :, :],
-                    func=ACTF.Exp, bias=nb[:], scale=-1.0, accum_out=den[:, r, 1:2])
+                    func=ACTF.Exp, bias=nb[:], scale=SCALE, accum_out=den[:, r, 1:2])
 
         def flip(key, bank, sources):
             et = psum.tile([P, len(sources), 2, P], F32, tag=bank, name="et")
@@ -296,15 +299,15 @@ def tile_slidingwindowattention_kernel(tc, q, k, v, out):
             flip(("w", bk, gi), bank, [ew_tile(bk, w[-1]) for w in groups(bk)[gi]])
 
         def evict_group(bk, gi):
-            evict(("w", bk, gi), len(groups(bk)[gi]), nc.scalar.copy)
+            evict(("w", bk, gi), len(groups(bk)[gi]))
 
         def quant_group(bk, gi):
             quant(("w", bk, gi), len(groups(bk)[gi]))
 
-        def evict(key, parts, copy):
+        def evict(key, parts):
             g = gpool.tile([P, parts, P, 4], BF16, tag="g%d" % parts, name="g", align_bytes=64)
             dst = g[:].rearrange("p a n t -> p (a n t)").bitcast(F32).rearrange("p (a n u) -> p a n u", a=parts, u=2)
-            copy(out=dst, in_=st[("et",) + key][:].rearrange("p a u n -> p a n u"))
+            nc.scalar.copy(out=dst, in_=st[("et",) + key][:].rearrange("p a u n -> p a n u"))
             st[("g",) + key] = g
 
         def quant(key, parts):
@@ -346,18 +349,19 @@ def tile_slidingwindowattention_kernel(tc, q, k, v, out):
 
         def den_sum(bk):
             h, j = blocks[bk]
+            den = st[("den", bk)]
+            if bk % 2 == 0:
+                st[("dsum", bk // 2)] = small.tile([P, 2, TPB], F32, tag="dsum", name="dsum")
+            dsum = st[("dsum", bk // 2)][:, bk % 2, :]
             if j > 0:
-                den = st[("den", bk)]
-                dsum = small.tile([P, TPB], F32, tag="dsum")
-                nc.gpsimd.tensor_tensor(out=dsum[:], in0=den[:, :, 0], in1=den[:, :, 1], op=ALU.add)
-                st[("dsum", bk)] = dsum[:]
+                nc.gpsimd.tensor_tensor(out=dsum, in0=den[:, :, 0], in1=den[:, :, 1], op=ALU.add)
             else:
-                st[("dsum", bk)] = st[("den", bk)][:, :, 0]
+                nc.gpsimd.tensor_scalar(out=dsum, in0=den[:, :, 0], scalar1=1.0, scalar2=0.0, op0=ALU.mult, op1=ALU.add)
 
-        def recip(bk):
-            rden = small.tile([P, TPB], F32, tag="rden")
-            nc.vector.reciprocal(out=rden[:], in_=st[("dsum", bk)])
-            st[("rden", bk)] = rden
+        def recip(pair):
+            rden = small.tile([P, 2, TPB], F32, tag="rden")
+            nc.vector.reciprocal(out=rden[:], in_=st[("dsum", pair)][:])
+            st[("rden", pair)] = rden
 
         def fin(bk, gis=(0, 1)):
             h, j = blocks[bk]
@@ -366,7 +370,7 @@ def tile_slidingwindowattention_kernel(tc, q, k, v, out):
             res = opool.tile([P, TPB, D], F32, tag="res")
             nc.vector.tensor_tensor(
                 out=res[:, p0:p1, :], in0=st[("acc", bk, gis[-1])][:, p0:p1, :],
-                in1=st[("rden", bk)][:, p0:p1].unsqueeze(2).to_broadcast([P, p1 - p0, D]), op=ALU.mult)
+                in1=st[("rden", bk // 2)][:, bk % 2, p0:p1].unsqueeze(2).to_broadcast([P, p1 - p0, D]), op=ALU.mult)
             rows = out[0, h, j * W:(j + 1) * W, :]
             if j > 0:
                 nc.sync.dma_start(out=rows.rearrange("(r p) d -> p r d", p=P), in_=res[:])
@@ -376,12 +380,12 @@ def tile_slidingwindowattention_kernel(tc, q, k, v, out):
 
         preps = {
             -1: [(0, 0, 4, 4, "bankB")],
-            0: [(0, 1, 4, 4, "sl1"), (0, 0, 8, 8, "sl0")],
-            2: [(0, 1, 8, 8, "sl0")],
-            4: [(1, 0, 0, 8, "bankA")],
-            5: [(1, 1, 0, 8, "sl0")],
-            6: [(1, 0, 8, 8, "bankA")],
-            8: [(1, 1, 8, 8, "bankA")],
+            0: [(0, 1, 4, 4, "sl1")],
+            3: [(0, 0, 8, 8, "bankA")],
+            4: [(0, 1, 8, 8, "sl0")],
+            5: [(1, 0, 0, 8, "bankA"), (1, 1, 0, 8, "sl0")],
+            7: [(1, 0, 8, 8, "bankA")],
+            9: [(1, 1, 8, 8, "bankA")],
         }
         for h in range(2, H):
             s0 = TPH * (h - 1)
@@ -389,9 +393,6 @@ def tile_slidingwindowattention_kernel(tc, q, k, v, out):
             preps[s0 - 1] = [(h, 1, 0, 8, "sl0")]
             preps[s0 + 1] = [(h, 0, 8, 8, "sl0")]
             preps[s0 + 3] = [(h, 1, 8, 8, "sl0")]
-
-        def lead_on_vector(bk):
-            return blocks[bk][1] >= 2
 
         def slot(s):
             r = s % TPB
@@ -408,17 +409,19 @@ def tile_slidingwindowattention_kernel(tc, q, k, v, out):
                 evict_group(bk - 1, 0)
             if r == 2 and has(bk - 1):
                 evict_group(bk - 1, 1)
-            if r == 3 and has(bk - 1, True) and not lead_on_vector(bk - 1):
-                evict(("l", bk - 1), 1, nc.scalar.copy)
+            if r == 3 and has(bk - 1, True):
+                evict(("l", bk - 1), 1)
             for args in preps.get(s - 1, []):
-                if args[1] == 1:
+                if not prep_on_vector(*args[:3]):
                     prep_copy(*args[:4])
+            if s in (1, 2):
+                regroup(0, s + 1, s + 2, 0, D, on_scalar=True)
             if s + 2 < len(tiles):
                 scores(s + 2)
             if r == 3 and has(bk):
                 flip_group(bk, 0, "bankB")
             if r == 1 and has(bk - 1):
-                flip_group(bk - 1, 1, "bankB")
+                flip_group(bk - 1, 1, "sw0" if bk - 1 == last else "bankB")
             if r == 2 and has(bk - 1, True):
                 flip(("l", bk - 1), "bankA", [st[("el", bk - 1)]])
             if r == 2 and has(bk + 1, True):
@@ -429,58 +432,53 @@ def tile_slidingwindowattention_kernel(tc, q, k, v, out):
                 mx(last - 1)
             if s == TPB * last + 7:
                 mx(last, (0,), "bankB")
-            if s == TPB * last + 8:
-                mx(last, (1,))
+                mx(last, (1,), "sw1")
             for args in preps.get(s, []):
                 prep_pe(*args)
             if s + 1 < len(tiles):
-                window_min(s + 1)
+                window_max(s + 1)
             if r == 3 and has(bk + 1, True):
-                lead_min(bk + 1)
+                lead_max(bk + 1)
+            if s == TPB * last + 6:
+                recip(last // 2)
             if r == 2 and has(bk - 1):
                 quant_group(bk - 1, 0)
             if r == 0 and has(bk - 2) and bk - 2 < last:
                 quant_group(bk - 2, 1)
                 if has(bk - 2, True):
                     quant(("l", bk - 2), 1)
-            if s == TPB * last + 7:
-                quant_group(last, 1)
-            if r == 3 and has(bk - 1):
-                recip(bk - 1)
+            if r == 3 and has(bk - 1) and bk % 2 == 0 and bk - 1 < last:
+                recip((bk - 1) // 2)
             for args in preps.get(s - 1, []):
-                if args[1] == 0:
+                if prep_on_vector(*args[:3]):
                     prep_copy(*args[:4])
             if r == 1 and has(bk - 3) and bk - 3 < last - 1:
                 fin(bk - 3)
             if s == TPB * last + 6:
+                quant_group(last, 1)
                 fin(last - 1)
-            if s == TPB * last + 8:
+            if s == TPB * last + 7:
                 fin(last, (0,))
-            if s == TPB * last + 9:
                 fin(last, (1,))
-            if r == 3 and has(bk - 1, True) and lead_on_vector(bk - 1):
-                evict(("l", bk - 1), 1, nc.vector.tensor_copy)
             if s + 1 < len(tiles):
                 join(s + 1)
-            if r == 2 and has(bk - 1):
+            if r == 1 and has(bk - 1):
                 den_sum(bk - 1)
             if s in (0, 1):
-                regroup(0, "vector", 2 * s, 2 * s + 2, 0, D)
-            if s == 2:
+                regroup(0, s, s + 1, 0, D)
+            if s == NB:
                 quant_v(0, 0, NB)
                 spread_v(0)
             if h + 1 < H:
-                if h == 0 and 5 <= hs <= 12:
-                    b, half = (hs - 5) // 2, (hs - 5) % 2
-                    regroup(1, "gpsimd", b, b + 1, half * (D // 2), (half + 1) * (D // 2))
-                if h > 0 and hs < NB:
-                    regroup(h + 1, "gpsimd", hs, hs + 1, 0, D)
+                if 3 <= hs <= 10:
+                    b, half = (hs - 3) // 2, (hs - 3) % 2
+                    regroup(h + 1, b, b + 1, half * (D // 2), (half + 1) * (D // 2))
                 if hs == 13:
                     quant_v(h + 1, 0, 2)
                 if hs == 15:
                     quant_v(h + 1, 2, 4)
                     spread_v(h + 1)
-            if hs == 0 and h + 2 < H:
+            if hs == NB and h + 2 < H:
                 load(h + 2)
 
         prep_pe(0, 0, 0, 4, "sl0")
@@ -489,7 +487,8 @@ def tile_slidingwindowattention_kernel(tc, q, k, v, out):
         prep_copy(0, 1, 0, 4)
         scores(0)
         scores(1)
-        window_min(0)
+        window_max(0)
+        join(0)
         prep_pe(*preps[-1][0])
-        for s in range(len(tiles) + 6):
+        for s in range(len(tiles) + 4):
             slot(s)

from contextlib import ExitStack

import concourse.mybir as mybir
from concourse.masks import make_identity

FP8X4 = mybir.dt.float8_e4m3fn_x4
BF16 = mybir.dt.bfloat16
F32 = mybir.dt.float32
I32 = mybir.dt.int32
U32 = mybir.dt.uint32
U8 = mybir.dt.uint8
ALU = mybir.AluOpType
ACTF = mybir.ActivationFunctionType
AX = mybir.AxisListType
ET = mybir.EngineType

H = 8
N = 2048
D = 128
W = 512
P = 128
NB = N // W
TPB = W // P
TPH = N // P
Q = P // TPB
SCALE = 0.125
BIG = 2.0 ** 100
FLOPS = 2 * 2 * H * (2 * NB - 1) * W * W * D
N_EW = 8
GROUPS = (((0,), (1,)), ((2,), (3,)))
GROUPS_FIRST = (((0, 2),), ((1,), (3,)))
GROUPS_LAST = (((1,), (3,)), ((0, 2),))
ACC_FIRST = (0, 2, 1, 3)


def tile_slidingwindowattention_kernel(tc, q, k, v, out):
    nc = tc.nc
    with ExitStack() as ctx:
        const = ctx.enter_context(tc.tile_pool(name="const", bufs=1))
        raw = ctx.enter_context(tc.tile_pool(name="raw", bufs=3))
        tpose = ctx.enter_context(tc.tile_pool(name="tpose", bufs=3))
        vpool = ctx.enter_context(tc.tile_pool(name="vpool", bufs=2))
        elpool = ctx.enter_context(tc.tile_pool(name="elpool", bufs=3))
        gpool = ctx.enter_context(tc.tile_pool(name="gpool", bufs=4))
        cpool = ctx.enter_context(tc.tile_pool(name="cpool", bufs=6))
        small = ctx.enter_context(tc.tile_pool(name="small", bufs=8))
        opool = ctx.enter_context(tc.tile_pool(name="opool", bufs=6))
        psum = ctx.enter_context(tc.psum_pool(name="psum", bufs=1))
        ctx.enter_context(tc.manual_schedule(engines={ET.PE, ET.Activation, ET.DVE, ET.Pool}))

        def zero(ap):
            nc.vector.memset(ap.bitcast(I32), 0)

        dummy = const.tile([P, 2], F32)
        nc.vector.memset(dummy[:], 0.0)
        nc.scalar.activation(out=dummy[:, 1:2], in_=dummy[:, 0:1], func=ACTF.Exp)

        ident = const.tile([P, P], BF16)
        make_identity(nc, ident[:])
        mask = const.tile([P, 2, P], BF16)
        nc.vector.memset(mask[:], 0.0)
        nc.gpsimd.affine_select(
            out=mask[:, 0, :], in_=mask[:, 0, :], compare_op=ALU.is_ge, fill=-BIG,
            base=0, pattern=[[-1, 2], [-4, Q], [-2, 2]], channel_multiplier=1,
        )
        nc.gpsimd.affine_select(
            out=mask[:, 1, :], in_=mask[:, 1, :], compare_op=ALU.is_ge, fill=-BIG,
            base=-1, pattern=[[1, 2], [4, Q], [2, 2]], channel_multiplier=-1,
        )
        mask_v = mask[:].rearrange("p m (u x) -> p m u x", u=2)
        ident_f = const.tile([P, P], F32)
        make_identity(nc, ident_f[:])

        heads = {}
        st = {}

        def load_raw(h):
            hd = {
                "qr": raw.tile([P, N // P, D], BF16, tag="qr", name="qr"),
                "kr": raw.tile([P, N // P, D], BF16, tag="kr", name="kr"),
                "vr": raw.tile([P, N // P, D], BF16, tag="vr", name="vr"),
            }
            heads[h] = hd

        def load_q(h, t0, t1):
            rows = q[0, h].rearrange("(g p) d -> p g d", p=P)
            nc.sync.dma_start(out=heads[h]["qr"][:, t0:t1, :], in_=rows[:, t0:t1, :])

        def load_k(h, t0, t1):
            rows = k[0, h].rearrange("(g p s) d -> p g (s d)", p=P, s=2)
            dst = heads[h]["kr"][:].rearrange("p (g s) d -> p g (s d)", s=2)
            nc.sync.dma_start(out=dst[:, t0 // 2:t1 // 2, :], in_=rows[:, t0 // 2:t1 // 2, :])

        def load_v(h):
            rows = v[0, h].rearrange("(b p t) d -> p b (t d)", p=P, t=4)
            nc.sync.dma_start(out=heads[h]["vr"][:].rearrange("p (b t) d -> p b (t d)", t=4), in_=rows)

        def load(h):
            load_raw(h)
            load_v(h)
            load_q(h, 0, 8)
            load_k(h, 0, 8)
            load_q(h, 8, 16)
            load_k(h, 8, 16)

        load_raw(0)
        load_q(0, 0, 4)
        load_k(0, 0, 4)
        load_q(0, 4, 8)
        load_k(0, 4, 8)
        load_v(0)
        load_q(0, 8, 16)
        load_k(0, 8, 16)
        load(1)

        vsets = []

        def make_vset(i):
            vset = {
                "vq": const.tile([P, NB, D], U32, name="vq%d" % i, align_bytes=64),
                "vs": const.tile([P, NB, D], U8, name="vs%d" % i, align_bytes=64),
                "vwc": const.tile([P, TPB - 1, NB, D], U32, name="vwc%d" % i, align_bytes=64),
                "vws": const.tile([P, TPB - 1, NB, D], U8, name="vws%d" % i, align_bytes=64),
                "vbc": const.tile([P, NB - 1, TPB, D], U32, name="vbc%d" % i, align_bytes=64),
                "vbs": const.tile([P, NB - 1, TPB, D], U8, name="vbs%d" % i, align_bytes=64),
                "vpc": const.tile([P, 2, D], U32, name="vpc%d" % i, align_bytes=64),
                "vps": const.tile([P, 2, D], U8, name="vps%d" % i, align_bytes=64),
            }
            zero(vset["vs"][:].rearrange("p b d -> p (b d)"))
            zero(vset["vwc"][:, 1, 0, :])
            zero(vset["vws"][:, 1, 0, :])
            zero(vset["vpc"][:].rearrange("p a d -> p (a d)"))
            zero(vset["vps"][:].rearrange("p a d -> p (a d)"))
            zero(vset["vbc"][:].rearrange("p a b d -> p (a b d)"))
            zero(vset["vbs"][:].rearrange("p a b d -> p (a b d)"))
            vsets.append(vset)

        make_vset(0)
        ew_tiles = []
        for i in range(N_EW):
            ew0 = const.tile([P, 2, 2 * P], BF16, name="ew%d" % i)
            ew_tiles.append(ew0)
        zero(ew_tiles[1][:].rearrange("p u x -> p (u x)"))
        make_vset(1)

        def prep_pe(h, which, t0, n, bank):
            src = heads[h]["qr" if which == 0 else "kr"]
            pt = psum.tile([P, 8 * P], BF16, tag=bank, name="pt")
            for i in range(n):
                t = t0 + i
                if which == 1:
                    b, u, hh = t // 4, (t // 2) % 2, t % 2
                    t = 4 * b + 2 * hh + u
                nc.tensor.transpose(pt[:, i * P:(i + 1) * P], src[:, t, :], ident[:])
            st[("pt", h, which, t0)] = pt

        def prep_on_vector(h, which, t0):
            return which == 0 and (h % 2 or t0 < 8)

        def prep_copy(h, which, t0, n):
            nm = "qT" if which == 0 else "kT"
            if t0 == 0:
                heads[h][nm] = tpose.tile([P, N], BF16, tag=nm, name=nm)
            dst = heads[h][nm][:, P * t0:P * (t0 + n)]
            pt = st[("pt", h, which, t0)]
            copy = nc.vector.tensor_copy if prep_on_vector(h, which, t0) else nc.scalar.copy
            copy(out=dst, in_=pt[:, 0:n * P])

        def regroup(h, b0, b1, d0, d1, on_scalar=False):
            if "vg" not in heads[h]:
                heads[h]["vg"] = vpool.tile([P, NB, D, 4], BF16, tag="vg", name="vg", align_bytes=64)
            dst = heads[h]["vg"][:].rearrange("p b d (u e) -> p b d u e", e=2)
            src = heads[h]["vr"][:].rearrange("p (b e u) d -> p b d u e", e=2, u=2)
            for b in range(b0, b1):
                if on_scalar:
                    nc.scalar.copy(out=dst[:, b, d0:d1], in_=src[:, b, d0:d1])
                else:
                    nc.gpsimd.tensor_scalar(out=dst[:, b, d0:d1], in0=src[:, b, d0:d1], scalar1=1.0, scalar2=0.0, op0=ALU.mult, op1=ALU.add)

        def quant_v(h, b0, b1):
            vset = vsets[h % 2]
            vg = heads[h]["vg"]
            nc.vector.quantize_mx(
                out=vset["vq"][:, b0:b1, :].rearrange("p b d -> p (b d)").bitcast(FP8X4),
                scales=vset["vs"][:, b0:b1, :].rearrange("p b d -> p (b d)"),
                in_=vg[:, b0:b1, :, :].rearrange("p b d t -> p (b d t)"),
            )

        def spread_v(h):
            vset = vsets[h % 2]
            for src_n, win_n, bd_n, pk_n in (("vq", "vwc", "vbc", "vpc"), ("vs", "vws", "vbs", "vps")):
                src = vset[src_n][:].bitcast(I32)
                win = vset[win_n][:].bitcast(I32)
                bd = vset[bd_n][:].bitcast(I32)
                pk = vset[pk_n][:].bitcast(I32)
                nc.sync.dma_start(out=pk[3 * Q:P, 0, :], in_=src[0:Q, 0, :])
                nc.sync.dma_start(out=pk[0:3 * Q, 1, :], in_=src[0:3 * Q, 0, :])
                for r in range(TPB - 1):
                    cut = Q * (r + 1)
                    b0 = 0 if r == 1 else 1
                    nc.sync.dma_start(out=win[0:cut, r, b0:NB, :], in_=src[0:cut, b0:NB, :])
                    nc.sync.dma_start(out=win[cut:P, r, 1:NB, :], in_=src[cut:P, 0:NB - 1, :])
                for s in range(TPB):
                    nc.sync.dma_start(out=bd[Q * s:Q * (s + 1), :, s, :], in_=src[Q * s:Q * (s + 1), 0:NB - 1, :])

        blocks = [(h, j) for h in range(H - 1) for j in range(NB)] + [(H - 1, j) for j in (1, 2, 3, 0)]
        last = len(blocks) - 1

        def groups(bk):
            return GROUPS if blocks[bk][1] > 0 else GROUPS_LAST if bk == last else GROUPS_FIRST

        tiles = [(h, j, r) for bk, (h, j) in enumerate(blocks) for g in groups(bk) for w in g for r in w]

        def kT_view(h):
            return heads[h]["kT"][:].rearrange("d (b u x) -> d b u x", u=2, x=2 * P)

        def lead_scores(bk):
            h, j = blocks[bk]
            hd = heads[h]
            sl = psum.tile([P, TPB, 2, 2 * Q], F32, tag="sl%d" % (bk % 2), name="sl")
            for r in range(TPB):
                i = TPB * j + r
                nc.tensor.matmul(sl[:, r, :, :], lhsT=hd["qT"][:, i * P:(i + 1) * P], rhs=kT_view(h)[:, j - 1, :, 2 * Q * r:2 * Q * (r + 1)], start=True, stop=False)
                nc.tensor.matmul(sl[:, r, :, :], lhsT=ident[:], rhs=mask_v[:, 1, :, :], start=False, stop=True)
            st[("sl", bk)] = sl

        def lead_max(bk):
            mxl = small.tile([P, TPB], F32, tag="mxl")
            nc.vector.tensor_reduce(out=mxl[:], in_=st[("sl", bk)][:].rearrange("p r u x -> p r (u x)"), axis=AX.X, op=ALU.max)
            st[("mxl", bk)] = mxl

        def scores(x):
            h, j, r = tiles[x]
            i = TPB * j + r
            qcols = heads[h]["qT"][:, i * P:(i + 1) * P]
            cut = 2 * Q * (r + 1)
            sw = psum.tile([P, 2, 2 * P], F32, tag="sw%d" % (x % 4), name="sw")
            nc.tensor.matmul(sw[:, :, 0:cut], lhsT=qcols, rhs=kT_view(h)[:, j, :, 0:cut], start=True, stop=False)
            if j > 0 and cut < 2 * P:
                nc.tensor.matmul(sw[:, :, cut:2 * P], lhsT=qcols, rhs=kT_view(h)[:, j - 1, :, cut:2 * P], start=False, stop=False)
            nc.tensor.matmul(sw[:, :, cut - 2 * Q:cut], lhsT=ident[:], rhs=mask_v[:, 0, :, :], start=False, stop=True)
            st[("sw", x)] = sw

        def seen(x):
            h, j, r = tiles[x]
            return 2 * P if j > 0 else 2 * Q * (r + 1)

        def window_max(x):
            mxw = small.tile([P, 1], F32, tag="mxw")
            sw = st[("sw", x)]
            if seen(x) == 2 * P:
                nc.vector.tensor_reduce(out=mxw[:], in_=sw[:].rearrange("p u x -> p (u x)"), axis=AX.X, op=ALU.max)
            else:
                nc.vector.tensor_reduce(out=mxw[:], in_=sw[:, :, 0:seen(x)], axis=AX.XY, op=ALU.max)
            st[("mx", x)] = mxw

        def join(x):
            h, j, r = tiles[x]
            nb = small.tile([P, 1], F32, tag="nb")
            if j > 0:
                nc.gpsimd.tensor_scalar(out=nb[:], in0=st[("mx", x)][:], scalar1=st[("mxl", x // TPB)][:, r:r + 1], scalar2=-SCALE, op0=ALU.max, op1=ALU.mult)
            else:
                nc.gpsimd.tensor_scalar(out=nb[:], in0=st[("mx", x)][:], scalar1=-SCALE, scalar2=0.0, op0=ALU.mult, op1=ALU.add)
            st[("nb", x)] = nb

        def ew_tile(bk, r):
            return ew_tiles[(TPB * bk + r) % N_EW]

        def place(bk, r):
            return r if blocks[bk][1] > 0 else ACC_FIRST.index(r)

        def expo(x):
            h, j, r = tiles[x]
            bk = x // TPB
            nb = st[("nb", x)]
            if x % TPB == 0:
                st[("den", bk)] = small.tile([P, TPB, 2], F32, tag="den", name="den")
                if j > 0:
                    st[("el", bk)] = elpool.tile([P, 2, 2 * P], BF16, tag="el", name="el")
            den = st[("den", bk)]
            r_to, c_to = (2, 3 * 2 * Q) if (j, r) == (0, 0) else (r, 0)
            nc.scalar.activation(
                out=ew_tile(bk, r_to)[:, :, c_to:c_to + seen(x)], in_=st[("sw", x)][:, :, 0:seen(x)],
                func=ACTF.Exp, bias=nb[:], scale=SCALE, accum_out=den[:, place(bk, r), 0:1])
            if j > 0:
                nc.scalar.activation(
                    out=st[("el", bk)][:, :, 2 * Q * r:2 * Q * (r + 1)], in_=st[("sl", bk)][:, r, :, :],
                    func=ACTF.Exp, bias=nb[:], scale=SCALE, accum_out=den[:, r, 1:2])

        def flip(key, bank, sources):
            et = psum.tile([P, len(sources), 2, P], F32, tag=bank, name="et")
            for a, src in enumerate(sources):
                words = src[:].rearrange("p u x -> p (u x)").bitcast(F32)
                for u in range(2):
                    nc.tensor.transpose(et[:, a, u, :], words[:, u * P:(u + 1) * P], ident_f[:])
            st[("et",) + key] = et

        def flip_group(bk, gi, bank):
            flip(("w", bk, gi), bank, [ew_tile(bk, w[-1]) for w in groups(bk)[gi]])

        def evict_group(bk, gi):
            evict(("w", bk, gi), len(groups(bk)[gi]))

        def quant_group(bk, gi):
            quant(("w", bk, gi), len(groups(bk)[gi]))

        def evict(key, parts):
            g = gpool.tile([P, parts, P, 4], BF16, tag="g%d" % parts, name="g", align_bytes=64)
            dst = g[:].rearrange("p a n t -> p (a n t)").bitcast(F32).rearrange("p (a n u) -> p a n u", a=parts, u=2)
            nc.scalar.copy(out=dst, in_=st[("et",) + key][:].rearrange("p a u n -> p a n u"))
            st[("g",) + key] = g

        def quant(key, parts):
            g = st[("g",) + key]
            codes = cpool.tile([P, parts * P], U32, tag="codes%d" % parts, name="codes", align_bytes=64)
            scl = cpool.tile([P, parts * P], U8, tag="scl%d" % parts, name="scl", align_bytes=64)
            nc.vector.quantize_mx(out=codes[:].bitcast(FP8X4), scales=scl[:], in_=g[:].rearrange("p a n t -> p (a n t)"))
            st[("c",) + key] = (codes, scl)

        def mx(bk, gis=(0, 1), bank="bankA"):
            h, j = blocks[bk]
            vset = vsets[h % 2]
            acc = psum.tile([P, TPB, D], F32, tag=bank, name="acc")
            for gi in gis:
                codes, scl = st[("c", "w", bk, gi)]
                for a, w in enumerate(groups(bk)[gi]):
                    r = w[-1]
                    cols = slice(a * P, (a + 1) * P)
                    if len(w) == 2:
                        rhs, rsc = vset["vpc"][:].rearrange("p a d -> p (a d)"), vset["vps"][:].rearrange("p a d -> p (a d)")
                    elif r < TPB - 1:
                        rhs, rsc = vset["vwc"][:, r, j, :], vset["vws"][:, r, j, :]
                    else:
                        rhs, rsc = vset["vq"][:, j, :], vset["vs"][:, j, :]
                    p0 = place(bk, w[0])
                    nc.tensor.matmul_mx(
                        out=acc[:, p0:p0 + len(w), :].rearrange("p r d -> p (r d)"),
                        lhsT=codes[:, cols].bitcast(FP8X4), lhsT_scale=scl[:, cols],
                        rhs=rhs.bitcast(FP8X4), rhs_scale=rsc,
                        start=(j == 0 or r == 0), stop=(j == 0))
            if j > 0:
                codes, scl = st[("c", "l", bk)]
                nc.tensor.matmul_mx(
                    out=acc[:].rearrange("p r d -> p (r d)"), lhsT=codes[:].bitcast(FP8X4), lhsT_scale=scl[:],
                    rhs=vset["vbc"][:, j - 1, :, :].rearrange("p s d -> p (s d)").bitcast(FP8X4),
                    rhs_scale=vset["vbs"][:, j - 1, :, :].rearrange("p s d -> p (s d)"),
                    start=False, stop=True)
            st[("acc", bk, gis[-1])] = acc

        def den_sum(bk):
            h, j = blocks[bk]
            den = st[("den", bk)]
            if bk % 2 == 0:
                st[("dsum", bk // 2)] = small.tile([P, 2, TPB], F32, tag="dsum", name="dsum")
            dsum = st[("dsum", bk // 2)][:, bk % 2, :]
            if j > 0:
                nc.gpsimd.tensor_tensor(out=dsum, in0=den[:, :, 0], in1=den[:, :, 1], op=ALU.add)
            else:
                nc.gpsimd.tensor_scalar(out=dsum, in0=den[:, :, 0], scalar1=1.0, scalar2=0.0, op0=ALU.mult, op1=ALU.add)

        def recip(pair):
            rden = small.tile([P, 2, TPB], F32, tag="rden")
            nc.vector.reciprocal(out=rden[:], in_=st[("dsum", pair)][:])
            st[("rden", pair)] = rden

        def fin(bk, gis=(0, 1)):
            h, j = blocks[bk]
            used = [place(bk, r) for gi in gis for w in groups(bk)[gi] for r in w]
            p0, p1 = min(used), max(used) + 1
            res = opool.tile([P, TPB, D], F32, tag="res")
            nc.vector.tensor_tensor(
                out=res[:, p0:p1, :], in0=st[("acc", bk, gis[-1])][:, p0:p1, :],
                in1=st[("rden", bk // 2)][:, bk % 2, p0:p1].unsqueeze(2).to_broadcast([P, p1 - p0, D]), op=ALU.mult)
            rows = out[0, h, j * W:(j + 1) * W, :]
            if j > 0:
                nc.sync.dma_start(out=rows.rearrange("(r p) d -> p r d", p=P), in_=res[:])
            else:
                for a in range(p0 // 2, p1 // 2):
                    nc.sync.dma_start(out=rows.rearrange("(b a p) d -> a p b d", a=2, p=P)[a], in_=res[:, 2 * a:2 * a + 2, :])

        preps = {
            -1: [(0, 0, 4, 4, "bankB")],
            0: [(0, 1, 4, 4, "sl1")],
            3: [(0, 0, 8, 8, "bankA")],
            4: [(0, 1, 8, 8, "sl0")],
            5: [(1, 0, 0, 8, "bankA"), (1, 1, 0, 8, "sl0")],
            7: [(1, 0, 8, 8, "bankA")],
            9: [(1, 1, 8, 8, "bankA")],
        }
        for h in range(2, H):
            s0 = TPH * (h - 1)
            preps[s0 - 3] = [(h, 0, 0, 8, "sl0")]
            preps[s0 - 1] = [(h, 1, 0, 8, "sl0")]
            preps[s0 + 1] = [(h, 0, 8, 8, "sl0")]
            preps[s0 + 3] = [(h, 1, 8, 8, "sl0")]

        def slot(s):
            r = s % TPB
            bk = s // TPB
            h, hs = s // TPH, s % TPH
            inside = s < len(tiles)

            def has(b, lead=False):
                return 0 <= b < len(blocks) and (not lead or blocks[b][1] > 0)

            if 0 <= s - 1 < len(tiles):
                expo(s - 1)
            if r == 0 and has(bk - 1):
                evict_group(bk - 1, 0)
            if r == 2 and has(bk - 1):
                evict_group(bk - 1, 1)
            if r == 3 and has(bk - 1, True):
                evict(("l", bk - 1), 1)
            for args in preps.get(s - 1, []):
                if not prep_on_vector(*args[:3]):
                    prep_copy(*args[:4])
            if s in (1, 2):
                regroup(0, s + 1, s + 2, 0, D, on_scalar=True)
            if s + 2 < len(tiles):
                scores(s + 2)
            if r == 3 and has(bk):
                flip_group(bk, 0, "bankB")
            if r == 1 and has(bk - 1):
                flip_group(bk - 1, 1, "sw0" if bk - 1 == last else "bankB")
            if r == 2 and has(bk - 1, True):
                flip(("l", bk - 1), "bankA", [st[("el", bk - 1)]])
            if r == 2 and has(bk + 1, True):
                lead_scores(bk + 1)
            if r == 0 and has(bk - 3) and bk - 3 < last - 1:
                mx(bk - 3)
            if s == TPB * last + 5:
                mx(last - 1)
            if s == TPB * last + 7:
                mx(last, (0,), "bankB")
                mx(last, (1,), "sw1")
            for args in preps.get(s, []):
                prep_pe(*args)
            if s + 1 < len(tiles):
                window_max(s + 1)
            if r == 3 and has(bk + 1, True):
                lead_max(bk + 1)
            if s == TPB * last + 6:
                recip(last // 2)
            if r == 2 and has(bk - 1):
                quant_group(bk - 1, 0)
            if r == 0 and has(bk - 2) and bk - 2 < last:
                quant_group(bk - 2, 1)
                if has(bk - 2, True):
                    quant(("l", bk - 2), 1)
            if r == 3 and has(bk - 1) and bk % 2 == 0 and bk - 1 < last:
                recip((bk - 1) // 2)
            for args in preps.get(s - 1, []):
                if prep_on_vector(*args[:3]):
                    prep_copy(*args[:4])
            if r == 1 and has(bk - 3) and bk - 3 < last - 1:
                fin(bk - 3)
            if s == TPB * last + 6:
                quant_group(last, 1)
                fin(last - 1)
            if s == TPB * last + 7:
                fin(last, (0,))
                fin(last, (1,))
            if s + 1 < len(tiles):
                join(s + 1)
            if r == 1 and has(bk - 1):
                den_sum(bk - 1)
            if s in (0, 1):
                regroup(0, s, s + 1, 0, D)
            if s == NB:
                quant_v(0, 0, NB)
                spread_v(0)
            if h + 1 < H:
                if 3 <= hs <= 10:
                    b, half = (hs - 3) // 2, (hs - 3) % 2
                    regroup(h + 1, b, b + 1, half * (D // 2), (half + 1) * (D // 2))
                if hs == 13:
                    quant_v(h + 1, 0, 2)
                if hs == 15:
                    quant_v(h + 1, 2, 4)
                    spread_v(h + 1)
            if hs == NB and h + 2 < H:
                load(h + 2)

        prep_pe(0, 0, 0, 4, "sl0")
        prep_pe(0, 1, 0, 4, "bankA")
        prep_copy(0, 0, 0, 4)
        prep_copy(0, 1, 0, 4)
        scores(0)
        scores(1)
        window_max(0)
        join(0)
        prep_pe(*preps[-1][0])
        for s in range(len(tiles) + 4):
            slot(s)
